import numpy as np
import ml_dtypes


def mxq(x, axis, fmt="e4m3"):
    dtype, down = {"e4m3": (ml_dtypes.float8_e4m3fn, 7), "e5m2": (ml_dtypes.float8_e5m2, 14)}[fmt]
    v = np.moveaxis(np.asarray(x, np.float32).astype(ml_dtypes.bfloat16).astype(np.float64), axis, -1)
    blocks = v.reshape(v.shape[:-1] + (-1, 32))
    amax = np.abs(blocks).max(-1, keepdims=True)
    byte = np.maximum(np.where(amax > 0, np.frexp(amax)[1] - 1 + 127, 0) - down, 1)
    scale = np.exp2(byte - 127.0)
    codes = (blocks / scale).astype(np.float32).astype(dtype).astype(np.float64)
    return np.moveaxis((codes * scale).reshape(v.shape), -1, axis)


WIDE = False


def mx_kscale(k):
    if not WIDE:
        return np.ones(k)
    levels = np.array([10, -10, 5, -5, 0])
    a = np.random.permutation(np.resize(levels, k // 512 * 4)).reshape(k // 512, 4)
    idx = np.arange(k)
    return np.exp2(a[idx // 512, idx % 128 // 32])


BF16 = ml_dtypes.bfloat16


def bf(x):
    return np.asarray(x, np.float32).astype(BF16)


def f64(x):
    return np.asarray(x).astype(np.float64)


E2M1 = np.array([0.0, 0.5, 1.0, 1.5, 2.0, 3.0, 4.0, 6.0, -0.0, -0.5, -1.0, -1.5, -2.0, -3.0, -4.0, -6.0])


def pack_weight(w, fmt):
    k, n = w.shape
    w = f64(bf(w)).reshape(k // 32, 32, n)
    amax = np.abs(w).max(1)
    if fmt == "e4m3":
        byte = np.frexp(amax)[1] - 1 + 127 - 7
    else:
        mant, ex = np.frexp(amax / 6.0)
        byte = np.where(mant > 0.5, ex, ex - 1) + 127
    byte = np.clip(np.where(amax > 0, byte, 1), 1, 254)
    scaled = (w * np.exp2(127.0 - byte)[:, None, :]).reshape(k, n).astype(np.float32)
    by_word = np.ascontiguousarray(scaled.reshape(k // 512, 128, 4, n).transpose(0, 1, 3, 2))
    if fmt == "e4m3":
        words = by_word.astype(ml_dtypes.float8_e4m3fn).view(np.uint8)
    else:
        c = by_word.astype(ml_dtypes.float4_e2m1fn).view(np.uint8) & 0xF
        words = c[..., 0::2] | (c[..., 1::2] << 4)
    return np.ascontiguousarray(words), np.ascontiguousarray(byte.astype(np.uint8).reshape(k // 512, 16, n))


def unpack_weight(words, scales, fmt):
    g, p, n, _ = words.shape
    if fmt == "e4m3":
        vals = np.ascontiguousarray(words).view(ml_dtypes.float8_e4m3fn).astype(np.float64)
    else:
        nib = np.empty((g, p, n, 4), np.uint8)
        nib[..., 0::2] = words & 0xF
        nib[..., 1::2] = words >> 4
        vals = E2M1[nib]
    vals = vals * np.repeat(np.exp2(scales.astype(np.float64) - 127.0), 8, axis=1)[..., None]
    return vals.transpose(0, 1, 3, 2).reshape(g * 512, n)

def pack4(w):
    words, scales = pack_weight(w, "e2m1")
    return words.reshape(words.shape[0], 128, -1), scales


def unpack4(words, scales):
    return unpack_weight(words.reshape(words.shape[0], 128, -1, 2), scales, "e2m1")


B, N, C, F = 4, 32, 1024, 1024
EPS_STD = 1e-5


def setup_inputs():
    u, s = mx_kscale(C), mx_kscale(C)
    rows = np.concatenate([u, u, s])
    x = bf(np.random.standard_normal((B, N, C)) * u)
    e_enc = bf(np.random.standard_normal((B, N, N, C)) * s)
    words, scales = pack4(np.random.standard_normal((3 * C, F)) / np.sqrt(3 * C) / rows[:, None])
    b_pre = bf(np.random.standard_normal(F) * 0.3)
    return {"x": x,
            "e_enc": e_enc,
            "W_pre_words": words,
            "W_pre_scales": scales,
            "b_pre": b_pre}


def reference(x, e_enc, W_pre_words, W_pre_scales, b_pre):
    w = unpack4(W_pre_words, W_pre_scales)
    xq = mxq(f64(x), 2, "e4m3")
    tgt = xq @ w[:C]
    src = xq @ w[C:2 * C]
    edg = mxq(f64(e_enc), 3, "e4m3") @ w[2 * C:]
    m = tgt[:, :, None, :] + src[:, None, :, :] + edg + f64(b_pre)
    mean = m.mean(axis=2)
    mn = m.min(axis=2)
    mx = m.max(axis=2)
    var = (m * m).mean(axis=2) - mean * mean
    std = np.sqrt(np.maximum(var, 0.0) + EPS_STD)
    return np.concatenate([mean, mn, mx, std], axis=-1)

@@ -1,0 +1,266 @@
+from contextlib import ExitStack
+
+import concourse.mybir as mybir
+from concourse.masks import make_identity
+
+F32 = mybir.dt.float32
+BF16 = mybir.dt.bfloat16
+I32 = mybir.dt.int32
+U32 = mybir.dt.uint32
+U8 = mybir.dt.uint8
+FP8X4 = mybir.dt.float8_e4m3fn_x4
+FP4X4 = mybir.dt.float4_e2m1fn_x4
+ALU = mybir.AluOpType
+ACT = mybir.ActivationFunctionType
+AXIS = mybir.AxisListType
+
+B, N, C, F = 4, 32, 1024, 1024
+EPS_STD = 1e-5
+P = 128
+PACK = 4
+K_PASS = P * PACK
+G = C // K_PASS
+W_TARGET, W_SOURCE, W_EDGE = 0, G, 2 * G
+F_TILES = F // P
+CHUNK = 512
+TARGETS = CHUNK // N
+CHUNKS = B * N * N // CHUNK
+CHUNKS_PER_GRAPH = CHUNKS // B
+ROW_TILES = CHUNK // P
+WORDS = K_PASS // 2
+AGGREGATORS = 4
+BANK_TILES = CHUNK // P
+
+QUANTISE_BEHIND = 5
+COMBINE_BEHIND = 1
+STORE_BEHIND = 6
+
+FLOPS = 2 * (B * N * N + 2 * B * N) * C * F
+
+
+def tile_gnnlayer_pa_kernel(tc, x, e_enc, W_pre_words, W_pre_scales, b_pre, out):
+    nc = tc.nc
+    with ExitStack() as ctx:
+        ctx.enter_context(tc.manual_schedule())
+        keep = ctx.enter_context(tc.tile_pool(name="keep", bufs=1))
+        work = ctx.enter_context(tc.tile_pool(name="work", bufs=2))
+        psum_turn = ctx.enter_context(tc.psum_pool(name="psum_turn", bufs=2))
+        psum_msg = ctx.enter_context(tc.psum_pool(name="psum_msg", bufs=4))
+        psum_out = ctx.enter_context(tc.psum_pool(name="psum_out", bufs=2))
+
+        x_raw = keep.tile([P, C], BF16)
+        e_raw = keep.tile([P, CHUNKS, ROW_TILES, C], BF16)
+        w_words = keep.tile([P, 3 * G, 2 * F], U8, align_bytes=64)
+        w_scales = keep.tile([P, 3 * G, F], U8, align_bytes=64)
+        x_grouped = keep.tile([P, G, P, PACK], BF16, align_bytes=64)
+        x_codes = keep.tile([P, G, P], U32, align_bytes=64)
+        x_scales = keep.tile([P, G, P], U8, align_bytes=64)
+        src_codes = keep.tile([P, B, G, CHUNK], U32, align_bytes=64)
+        src_scales = keep.tile([P, B, G, CHUNK], U8, align_bytes=64)
+        ident = keep.tile([P, P], F32)
+        bias_rows_bf = keep.tile([P, P], BF16)
+        bias_rows = keep.tile([P, P], F32)
+        bias_col = keep.tile([P, F_TILES], F32)
+        base = keep.tile([P, F_TILES, B * N], F32)
+        eps = keep.tile([P, 1], F32)
+        warm = keep.tile([P, 1], F32)
+        squares = keep.tile([P, TARGETS, N], F32)
+
+        nc.vector.memset(w_scales[:].bitcast(I32), 0)
+        nc.vector.memset(x_scales[:].bitcast(I32), 0)
+        nc.vector.memset(bias_rows_bf[:], 0.0)
+        nc.vector.memset(eps[:], EPS_STD)
+        make_identity(nc, ident[:])
+        nc.scalar.activation(out=warm[:], in_=eps[:], func=ACT.Sqrt)
+
+        nc.sync.dma_start(out=x_raw[:], in_=x.rearrange("b n c -> (b n) c"))
+        edges = e_enc.rearrange("b i j c -> (b i j) c")
+
+        def load_chunk(c):
+            rows = edges[c * CHUNK : (c + 1) * CHUNK, :]
+            nc.sync.dma_start(out=e_raw[:, c, :, :], in_=rows.rearrange("(t p) c -> p t c", p=P))
+
+        load_chunk(0)
+        scale_rows = W_pre_scales.rearrange("g (h m r) n -> m r h g n", h=2, m=2, r=4)
+        for m in range(2):
+            for r in range(4):
+                nc.sync.dma_start(
+                    out=w_scales[32 * m + r : P : 64, :, :].bitcast(I32),
+                    in_=scale_rows[m, r].bitcast(I32),
+                )
+        nc.sync.dma_start(
+            out=w_words[:].bitcast(I32), in_=W_pre_words.rearrange("g p n -> p g n").bitcast(I32)
+        )
+        nc.sync.dma_start(out=bias_rows_bf[0:F_TILES, :], in_=b_pre.rearrange("(t f) -> t f", f=P))
+        for c in range(1, CHUNKS):
+            load_chunk(c)
+
+        def k_onto_partitions(rows_bf16, grouped):
+            words = rows_bf16.bitcast(F32)
+            turned = psum_turn.tile([P, G, 2, P], F32)
+            for g in range(G):
+                for u in range(2):
+                    nc.tensor.transpose(
+                        turned[:, g, u, :], words[:, g * WORDS + u : (g + 1) * WORDS : 2], ident[:]
+                    )
+            nc.scalar.copy(out=grouped.bitcast(F32), in_=turned[:].rearrange("p g u r -> p g r u"))
+
+        def weight(group, ft):
+            return dict(
+                lhsT=w_words[:, group, 2 * P * ft : 2 * P * (ft + 1)].bitcast(FP4X4),
+                lhsT_scale=w_scales[:, group, P * ft : P * (ft + 1)],
+            )
+
+        k_onto_partitions(x_raw[:], x_grouped[:])
+        nc.vector.quantize_mx(
+            out=x_codes[:].rearrange("p g r -> p (g r)").bitcast(FP8X4),
+            scales=x_scales[:].rearrange("p g r -> p (g r)"),
+            in_=x_grouped[:].rearrange("p g r t -> p (g r t)"),
+        )
+        for b in range(B):
+            nodes = slice(b * N, (b + 1) * N)
+            nc.vector.tensor_copy(
+                out=src_codes[:, b, :, :].bitcast(I32).rearrange("p g (i j) -> p g i j", j=N),
+                in_=x_codes[:, :, nodes].bitcast(I32).unsqueeze(2).to_broadcast([P, G, TARGETS, N]),
+            )
+            nc.vector.tensor_copy(
+                out=src_scales[:, b, :, :].bitcast(I32).rearrange("p g (i w) -> p g i w", w=N // 4),
+                in_=x_scales[:, :, nodes].bitcast(I32).unsqueeze(2).to_broadcast([P, G, TARGETS, N // 4]),
+            )
+
+        def new_chunk_tiles():
+            grouped = work.tile([P, G, CHUNK, PACK], BF16, align_bytes=64)
+            codes = work.tile([P, G, CHUNK], U32, align_bytes=64)
+            scales = work.tile([P, G, CHUNK], U8, align_bytes=64)
+            return grouped, codes, scales
+
+        def turn_row_tile(c, t, grouped):
+            k_onto_partitions(e_raw[:, c, t, :], grouped[:, :, t * P : (t + 1) * P, :])
+
+        def quantise_chunk(grouped, codes, scales):
+            nc.vector.quantize_mx(
+                out=codes[:].rearrange("p g e -> p (g e)").bitcast(FP8X4),
+                scales=scales[:].rearrange("p g e -> p (g e)"),
+                in_=grouped[:].rearrange("p g e t -> p (g e t)"),
+            )
+
+        following = new_chunk_tiles()
+        for t in range(ROW_TILES):
+            turn_row_tile(0, t, following[0])
+        quantise_chunk(*following)
+
+        nc.vector.tensor_copy(out=bias_rows[:], in_=bias_rows_bf[:])
+        bias_turned = psum_out.tile([P, BANK_TILES, P], F32, tag="bank")
+        nc.tensor.transpose(bias_turned[:, 0, :], bias_rows[:], ident[:])
+        nc.vector.tensor_copy(out=bias_col[:], in_=bias_turned[:, 0, 0:F_TILES])
+
+        for h in range(F_TILES // BANK_TILES):
+            target_term = psum_out.tile([P, BANK_TILES, P], F32, tag="bank")
+            for q in range(BANK_TILES):
+                for g in range(G):
+                    nc.tensor.matmul_mx(
+                        out=target_term[:, q, :],
+                        rhs=x_codes[:, g, :].bitcast(FP8X4),
+                        rhs_scale=x_scales[:, g, :],
+                        start=(g == 0),
+                        stop=(g == G - 1),
+                        **weight(W_TARGET + g, h * BANK_TILES + q),
+                    )
+            for q in range(BANK_TILES):
+                ft = h * BANK_TILES + q
+                nc.scalar.activation(
+                    out=base[:, ft, :],
+                    in_=target_term[:, q, :],
+                    func=ACT.Identity,
+                    bias=bias_col[:, ft : ft + 1],
+                    scale=1.0,
+                )
+
+        def aggregate(ft, b, codes, scales, stats, first_target):
+            s_sum, s_min, s_max, s_dev = stats
+            moving = [(W_SOURCE + g, src_codes[:, b, g, :], src_scales[:, b, g, :]) for g in range(G)]
+            moving += [(W_EDGE + g, codes[:, g, :], scales[:, g, :]) for g in range(G)]
+            bank = psum_msg.tile([P, CHUNK], F32)
+            for n, (group, rhs, rhs_scale) in enumerate(moving):
+                nc.tensor.matmul_mx(
+                    out=bank[:],
+                    rhs=rhs.bitcast(FP8X4),
+                    rhs_scale=rhs_scale,
+                    start=(n == 0),
+                    stop=(n == len(moving) - 1),
+                    **weight(group, ft),
+                )
+            s = bank[:].rearrange("p (i j) -> p i j", j=N)
+            targets = slice(first_target, first_target + TARGETS)
+            nc.vector.tensor_reduce(out=s_sum[:, ft, targets], in_=s, axis=AXIS.X, op=ALU.add)
+            nc.vector.tensor_reduce(out=s_max[:, ft, targets], in_=s, axis=AXIS.X, op=ALU.max)
+            nc.vector.tensor_reduce(out=s_min[:, ft, targets], in_=s, axis=AXIS.X, op=ALU.min)
+            for i in range(TARGETS):
+                column = slice(first_target + i, first_target + i + 1)
+                nc.scalar.activation(
+                    out=squares[:, i, :],
+                    in_=s[:, i, :],
+                    func=ACT.Square,
+                    bias=s_sum[:, ft, column],
+                    scale=-float(N),
+                    accum_out=s_dev[:, ft, column],
+                )
+
+        def combine_graph(b, stats):
+            s_sum, s_min, s_max, s_dev = stats
+            base_b = base[:, :, b * N : (b + 1) * N]
+            result = work.tile([P, F_TILES, AGGREGATORS, N], F32)
+            s_mean = work.tile([P, F_TILES, N], F32)
+            nc.gpsimd.tensor_scalar(
+                out=s_mean[:], in0=s_sum[:], scalar1=1.0 / N, scalar2=0.0, op0=ALU.mult, op1=ALU.add
+            )
+            nc.gpsimd.tensor_tensor(out=result[:, :, 0, :], in0=s_mean[:], in1=base_b, op=ALU.add)
+            nc.gpsimd.tensor_tensor(out=result[:, :, 1, :], in0=s_min[:], in1=base_b, op=ALU.add)
+            nc.gpsimd.tensor_tensor(out=result[:, :, 2, :], in0=s_max[:], in1=base_b, op=ALU.add)
+            nc.scalar.activation(
+                out=result[:, :, 3, :], in_=s_dev[:], func=ACT.Sqrt, bias=eps[:], scale=1.0 / (N * N * N)
+            )
+            return result
+
+        def store_graph(b, result):
+            rows = work.tile([P, F], F32)
+            for h in range(F_TILES // BANK_TILES):
+                turned = psum_out.tile([P, BANK_TILES, P], F32, tag="bank")
+                for q in range(BANK_TILES):
+                    nc.tensor.transpose(
+                        turned[:, q, :],
+                        result[:, h * BANK_TILES + q, :, :].rearrange("p a i -> p (a i)"),
+                        ident[:],
+                    )
+                nc.scalar.copy(
+                    out=rows[:, h * CHUNK : (h + 1) * CHUNK], in_=turned[:].rearrange("p q f -> p (q f)")
+                )
+            for a in range(AGGREGATORS):
+                nc.sync.dma_start(out=out[b, :, a * F : (a + 1) * F], in_=rows[a * N : (a + 1) * N, :])
+
+        stats = None
+        finished = None
+        result = None
+        for c in range(CHUNKS):
+            b, part = divmod(c, CHUNKS_PER_GRAPH)
+            if part == 0:
+                finished = stats
+                s_sum = work.tile([P, F_TILES, N], F32)
+                s_min = work.tile([P, F_TILES, N], F32)
+                s_max = work.tile([P, F_TILES, N], F32)
+                s_dev = work.tile([P, F_TILES, N], F32)
+                stats = (s_sum, s_min, s_max, s_dev)
+            current = following
+            if c + 1 < CHUNKS:
+                following = new_chunk_tiles()
+            for ft in range(F_TILES):
+                aggregate(ft, b, current[1], current[2], stats, part * TARGETS)
+                if c + 1 < CHUNKS and ft < ROW_TILES:
+                    turn_row_tile(c + 1, ft, following[0])
+                if c + 1 < CHUNKS and ft == QUANTISE_BEHIND:
+                    quantise_chunk(*following)
+                if part == 0 and b > 0 and ft == COMBINE_BEHIND:
+                    result = combine_graph(b - 1, finished)
+                if part == 0 and b > 0 and ft == STORE_BEHIND:
+                    store_graph(b - 1, result)
+        store_graph(B - 1, combine_graph(B - 1, stats))

@@ -30,9 +30,11 @@ ROW_TILES = CHUNK // P
 WORDS = K_PASS // 2
 AGGREGATORS = 4
 BANK_TILES = CHUNK // P
+SQUARE_BANKS = 4
 
 QUANTISE_BEHIND = 5
-COMBINE_BEHIND = 1
+REPEAT_BEHIND = 6
+COMBINE_BEHIND = 2
 STORE_BEHIND = 6
 
 FLOPS = 2 * (B * N * N + 2 * B * N) * C * F
@@ -64,7 +66,6 @@ def tile_gnnlayer_pa_kernel(tc, x, e_enc, W_pre_words, W_pre_scales, b_pre, out)
         base = keep.tile([P, F_TILES, B * N], F32)
         eps = keep.tile([P, 1], F32)
         warm = keep.tile([P, 1], F32)
-        squares = keep.tile([P, TARGETS, N], F32)
 
         nc.vector.memset(w_scales[:].bitcast(I32), 0)
         nc.vector.memset(x_scales[:].bitcast(I32), 0)
@@ -74,11 +75,20 @@ def tile_gnnlayer_pa_kernel(tc, x, e_enc, W_pre_words, W_pre_scales, b_pre, out)
         nc.scalar.activation(out=warm[:], in_=eps[:], func=ACT.Sqrt)
 
         nc.sync.dma_start(out=x_raw[:], in_=x.rearrange("b n c -> (b n) c"))
+        nc.sync.dma_start(out=bias_rows_bf[0:F_TILES, :], in_=b_pre.rearrange("(t f) -> t f", f=P))
         edges = e_enc.rearrange("b i j c -> (b i j) c")
 
         def load_chunk(c):
-            rows = edges[c * CHUNK : (c + 1) * CHUNK, :]
-            nc.sync.dma_start(out=e_raw[:, c, :, :], in_=rows.rearrange("(t p) c -> p t c", p=P))
+            for t in range(ROW_TILES):
+                first_row = c * CHUNK + t * P
+                nc.sync.dma_start(out=e_raw[:, c, t, :], in_=edges[first_row : first_row + P, :])
+
+        def load_weights(first_group, groups):
+            chosen = slice(first_group, first_group + groups)
+            nc.sync.dma_start(
+                out=w_words[:, chosen, :].bitcast(I32),
+                in_=W_pre_words[chosen].rearrange("g p n -> p g n").bitcast(I32),
+            )
 
         load_chunk(0)
         scale_rows = W_pre_scales.rearrange("g (h m r) n -> m r h g n", h=2, m=2, r=4)
@@ -88,11 +98,10 @@ def tile_gnnlayer_pa_kernel(tc, x, e_enc, W_pre_words, W_pre_scales, b_pre, out)
                     out=w_scales[32 * m + r : P : 64, :, :].bitcast(I32),
                     in_=scale_rows[m, r].bitcast(I32),
                 )
-        nc.sync.dma_start(
-            out=w_words[:].bitcast(I32), in_=W_pre_words.rearrange("g p n -> p g n").bitcast(I32)
-        )
-        nc.sync.dma_start(out=bias_rows_bf[0:F_TILES, :], in_=b_pre.rearrange("(t f) -> t f", f=P))
-        for c in range(1, CHUNKS):
+        load_weights(W_SOURCE, 2 * G)
+        load_chunk(1)
+        load_weights(W_TARGET, G)
+        for c in range(2, CHUNKS):
             load_chunk(c)
 
         def k_onto_partitions(rows_bf16, grouped):
@@ -112,12 +121,15 @@ def tile_gnnlayer_pa_kernel(tc, x, e_enc, W_pre_words, W_pre_scales, b_pre, out)
             )
 
         k_onto_partitions(x_raw[:], x_grouped[:])
+        nc.vector.tensor_copy(out=bias_rows[:], in_=bias_rows_bf[:])
+        bias_turned = psum_out.tile([P, BANK_TILES, P], F32, tag="bank")
+        nc.tensor.transpose(bias_turned[:, 0, :], bias_rows[:], ident[:])
         nc.vector.quantize_mx(
             out=x_codes[:].rearrange("p g r -> p (g r)").bitcast(FP8X4),
             scales=x_scales[:].rearrange("p g r -> p (g r)"),
             in_=x_grouped[:].rearrange("p g r t -> p (g r t)"),
         )
-        for b in range(B):
+        def repeat_sources(b):
             nodes = slice(b * N, (b + 1) * N)
             nc.vector.tensor_copy(
                 out=src_codes[:, b, :, :].bitcast(I32).rearrange("p g (i j) -> p g i j", j=N),
@@ -127,6 +139,9 @@ def tile_gnnlayer_pa_kernel(tc, x, e_enc, W_pre_words, W_pre_scales, b_pre, out)
                 out=src_scales[:, b, :, :].bitcast(I32).rearrange("p g (i w) -> p g i w", w=N // 4),
                 in_=x_scales[:, :, nodes].bitcast(I32).unsqueeze(2).to_broadcast([P, G, TARGETS, N // 4]),
             )
+
+        repeat_sources(0)
+        nc.vector.tensor_copy(out=bias_col[:], in_=bias_turned[:, 0, 0:F_TILES])
 
         def new_chunk_tiles():
             grouped = work.tile([P, G, CHUNK, PACK], BF16, align_bytes=64)
@@ -149,35 +164,31 @@ def tile_gnnlayer_pa_kernel(tc, x, e_enc, W_pre_words, W_pre_scales, b_pre, out)
             turn_row_tile(0, t, following[0])
         quantise_chunk(*following)
 
-        nc.vector.tensor_copy(out=bias_rows[:], in_=bias_rows_bf[:])
-        bias_turned = psum_out.tile([P, BANK_TILES, P], F32, tag="bank")
-        nc.tensor.transpose(bias_turned[:, 0, :], bias_rows[:], ident[:])
-        nc.vector.tensor_copy(out=bias_col[:], in_=bias_turned[:, 0, 0:F_TILES])
-
-        for h in range(F_TILES // BANK_TILES):
-            target_term = psum_out.tile([P, BANK_TILES, P], F32, tag="bank")
-            for q in range(BANK_TILES):
-                for g in range(G):
-                    nc.tensor.matmul_mx(
-                        out=target_term[:, q, :],
-                        rhs=x_codes[:, g, :].bitcast(FP8X4),
-                        rhs_scale=x_scales[:, g, :],
-                        start=(g == 0),
-                        stop=(g == G - 1),
-                        **weight(W_TARGET + g, h * BANK_TILES + q),
+        def target_terms():
+            for h in range(F_TILES // BANK_TILES):
+                target_term = psum_out.tile([P, BANK_TILES, P], F32, tag="bank")
+                for q in range(BANK_TILES):
+                    for g in range(G):
+                        nc.tensor.matmul_mx(
+                            out=target_term[:, q, :],
+                            rhs=x_codes[:, g, :].bitcast(FP8X4),
+                            rhs_scale=x_scales[:, g, :],
+                            start=(g == 0),
+                            stop=(g == G - 1),
+                            **weight(W_TARGET + g, h * BANK_TILES + q),
+                        )
+                for q in range(BANK_TILES):
+                    ft = h * BANK_TILES + q
+                    nc.scalar.activation(
+                        out=base[:, ft, :],
+                        in_=target_term[:, q, :],
+                        func=ACT.Identity,
+                        bias=bias_col[:, ft : ft + 1],
+                        scale=1.0,
                     )
-            for q in range(BANK_TILES):
-                ft = h * BANK_TILES + q
-                nc.scalar.activation(
-                    out=base[:, ft, :],
-                    in_=target_term[:, q, :],
-                    func=ACT.Identity,
-                    bias=bias_col[:, ft : ft + 1],
-                    scale=1.0,
-                )
 
-        def aggregate(ft, b, codes, scales, stats, first_target):
-            s_sum, s_min, s_max, s_dev = stats
+        def aggregate(ft, b, codes, scales, stats, squares, first_target):
+            s_sum, s_min, s_max = stats[0:3]
             moving = [(W_SOURCE + g, src_codes[:, b, g, :], src_scales[:, b, g, :]) for g in range(G)]
             moving += [(W_EDGE + g, codes[:, g, :], scales[:, g, :]) for g in range(G)]
             bank = psum_msg.tile([P, CHUNK], F32)
@@ -192,34 +203,43 @@ def tile_gnnlayer_pa_kernel(tc, x, e_enc, W_pre_words, W_pre_scales, b_pre, out)
                 )
             s = bank[:].rearrange("p (i j) -> p i j", j=N)
             targets = slice(first_target, first_target + TARGETS)
+            nc.scalar.activation(out=squares[:, ft % SQUARE_BANKS, :, :], in_=s, func=ACT.Square)
             nc.vector.tensor_reduce(out=s_sum[:, ft, targets], in_=s, axis=AXIS.X, op=ALU.add)
             nc.vector.tensor_reduce(out=s_max[:, ft, targets], in_=s, axis=AXIS.X, op=ALU.max)
             nc.vector.tensor_reduce(out=s_min[:, ft, targets], in_=s, axis=AXIS.X, op=ALU.min)
-            for i in range(TARGETS):
-                column = slice(first_target + i, first_target + i + 1)
-                nc.scalar.activation(
-                    out=squares[:, i, :],
-                    in_=s[:, i, :],
-                    func=ACT.Square,
-                    bias=s_sum[:, ft, column],
-                    scale=-float(N),
-                    accum_out=s_dev[:, ft, column],
+
+        def add_up_squares(squares, sums):
+            width = N // 2
+            while width > 1:
+                lower = squares[:, :, :, 0:width]
+                nc.gpsimd.tensor_tensor(
+                    out=lower, in0=lower, in1=squares[:, :, :, width : 2 * width], op=ALU.add
                 )
+                width = width // 2
+            nc.gpsimd.tensor_tensor(
+                out=sums, in0=squares[:, :, :, 0], in1=squares[:, :, :, 1], op=ALU.add
+            )
 
         def combine_graph(b, stats):
-            s_sum, s_min, s_max, s_dev = stats
+            s_sum, s_min, s_max, s_sq = stats
             base_b = base[:, :, b * N : (b + 1) * N]
             result = work.tile([P, F_TILES, AGGREGATORS, N], F32)
             s_mean = work.tile([P, F_TILES, N], F32)
+            spread = work.tile([P, F_TILES, N], F32)
             nc.gpsimd.tensor_scalar(
                 out=s_mean[:], in0=s_sum[:], scalar1=1.0 / N, scalar2=0.0, op0=ALU.mult, op1=ALU.add
+            )
+            nc.gpsimd.tensor_tensor(out=spread[:], in0=s_sum[:], in1=s_mean[:], op=ALU.mult)
+            nc.gpsimd.tensor_tensor(out=spread[:], in0=s_sq[:], in1=spread[:], op=ALU.subtract)
+            nc.gpsimd.tensor_scalar(
+                out=spread[:], in0=spread[:], scalar1=0.0, scalar2=0.0, op0=ALU.max, op1=ALU.add
+            )
+            nc.scalar.activation(
+                out=result[:, :, 3, :], in_=spread[:], func=ACT.Sqrt, bias=eps[:], scale=1.0 / N
             )
             nc.gpsimd.tensor_tensor(out=result[:, :, 0, :], in0=s_mean[:], in1=base_b, op=ALU.add)
             nc.gpsimd.tensor_tensor(out=result[:, :, 1, :], in0=s_min[:], in1=base_b, op=ALU.add)
             nc.gpsimd.tensor_tensor(out=result[:, :, 2, :], in0=s_max[:], in1=base_b, op=ALU.add)
-            nc.scalar.activation(
-                out=result[:, :, 3, :], in_=s_dev[:], func=ACT.Sqrt, bias=eps[:], scale=1.0 / (N * N * N)
-            )
             return result
 
         def store_graph(b, result):
@@ -241,24 +261,35 @@ def tile_gnnlayer_pa_kernel(tc, x, e_enc, W_pre_words, W_pre_scales, b_pre, out)
         stats = None
         finished = None
         result = None
+        squares = None
         for c in range(CHUNKS):
             b, part = divmod(c, CHUNKS_PER_GRAPH)
+            first_target = part * TARGETS
             if part == 0:
                 finished = stats
                 s_sum = work.tile([P, F_TILES, N], F32)
                 s_min = work.tile([P, F_TILES, N], F32)
                 s_max = work.tile([P, F_TILES, N], F32)
-                s_dev = work.tile([P, F_TILES, N], F32)
-                stats = (s_sum, s_min, s_max, s_dev)
+                s_sq = work.tile([P, F_TILES, N], F32)
+                stats = (s_sum, s_min, s_max, s_sq)
             current = following
             if c + 1 < CHUNKS:
                 following = new_chunk_tiles()
             for ft in range(F_TILES):
-                aggregate(ft, b, current[1], current[2], stats, part * TARGETS)
+                if ft % SQUARE_BANKS == 0:
+                    squares = work.tile([P, SQUARE_BANKS, TARGETS, N], F32)
+                aggregate(ft, b, current[1], current[2], stats, squares, first_target)
+                if ft % SQUARE_BANKS == SQUARE_BANKS - 1:
+                    tiles = slice(ft + 1 - SQUARE_BANKS, ft + 1)
+                    add_up_squares(squares, stats[3][:, tiles, first_target : first_target + TARGETS])
                 if c + 1 < CHUNKS and ft < ROW_TILES:
                     turn_row_tile(c + 1, ft, following[0])
                 if c + 1 < CHUNKS and ft == QUANTISE_BEHIND:
                     quantise_chunk(*following)
+                if part == CHUNKS_PER_GRAPH - 1 and b + 1 < B and ft == REPEAT_BEHIND:
+                    repeat_sources(b + 1)
+                if c == 0 and ft == COMBINE_BEHIND:
+                    target_terms()
                 if part == 0 and b > 0 and ft == COMBINE_BEHIND:
                     result = combine_graph(b - 1, finished)
                 if part == 0 and b > 0 and ft == STORE_BEHIND:

@@ -29,13 +29,12 @@ CHUNKS_PER_GRAPH = CHUNKS // B
 ROW_TILES = CHUNK // P
 WORDS = K_PASS // 2
 AGGREGATORS = 4
-BANK_TILES = CHUNK // P
-SQUARE_BANKS = 4
-
-QUANTISE_BEHIND = 5
-REPEAT_BEHIND = 6
-COMBINE_BEHIND = 2
-STORE_BEHIND = 6
+GROUP_TILES = CHUNK // P
+GROUPS_PER_CHUNK = F_TILES // GROUP_TILES
+GROUPS = CHUNKS * GROUPS_PER_CHUNK
+MOMENTS = 3
+FINISH_LAG = 2
+TARGET_TERMS_STEP = 1
 
 FLOPS = 2 * (B * N * N + 2 * B * N) * C * F
 
@@ -46,6 +45,7 @@ def tile_gnnlayer_pa_kernel(tc, x, e_enc, W_pre_words, W_pre_scales, b_pre, out)
         ctx.enter_context(tc.manual_schedule())
         keep = ctx.enter_context(tc.tile_pool(name="keep", bufs=1))
         work = ctx.enter_context(tc.tile_pool(name="work", bufs=2))
+        stream = ctx.enter_context(tc.tile_pool(name="stream", bufs=3))
         psum_turn = ctx.enter_context(tc.psum_pool(name="psum_turn", bufs=2))
         psum_msg = ctx.enter_context(tc.psum_pool(name="psum_msg", bufs=4))
         psum_out = ctx.enter_context(tc.psum_pool(name="psum_out", bufs=2))
@@ -120,15 +120,6 @@ def tile_gnnlayer_pa_kernel(tc, x, e_enc, W_pre_words, W_pre_scales, b_pre, out)
                 lhsT_scale=w_scales[:, group, P * ft : P * (ft + 1)],
             )
 
-        k_onto_partitions(x_raw[:], x_grouped[:])
-        nc.vector.tensor_copy(out=bias_rows[:], in_=bias_rows_bf[:])
-        bias_turned = psum_out.tile([P, BANK_TILES, P], F32, tag="bank")
-        nc.tensor.transpose(bias_turned[:, 0, :], bias_rows[:], ident[:])
-        nc.vector.quantize_mx(
-            out=x_codes[:].rearrange("p g r -> p (g r)").bitcast(FP8X4),
-            scales=x_scales[:].rearrange("p g r -> p (g r)"),
-            in_=x_grouped[:].rearrange("p g r t -> p (g r t)"),
-        )
         def repeat_sources(b):
             nodes = slice(b * N, (b + 1) * N)
             nc.vector.tensor_copy(
@@ -140,34 +131,25 @@ def tile_gnnlayer_pa_kernel(tc, x, e_enc, W_pre_words, W_pre_scales, b_pre, out)
                 in_=x_scales[:, :, nodes].bitcast(I32).unsqueeze(2).to_broadcast([P, G, TARGETS, N // 4]),
             )
 
-        repeat_sources(0)
-        nc.vector.tensor_copy(out=bias_col[:], in_=bias_turned[:, 0, 0:F_TILES])
-
-        def new_chunk_tiles():
+        def prepare_chunk(c):
             grouped = work.tile([P, G, CHUNK, PACK], BF16, align_bytes=64)
             codes = work.tile([P, G, CHUNK], U32, align_bytes=64)
             scales = work.tile([P, G, CHUNK], U8, align_bytes=64)
-            return grouped, codes, scales
-
-        def turn_row_tile(c, t, grouped):
-            k_onto_partitions(e_raw[:, c, t, :], grouped[:, :, t * P : (t + 1) * P, :])
-
-        def quantise_chunk(grouped, codes, scales):
+            for t in range(ROW_TILES):
+                k_onto_partitions(e_raw[:, c, t, :], grouped[:, :, t * P : (t + 1) * P, :])
+            if c % CHUNKS_PER_GRAPH == 0:
+                repeat_sources(c // CHUNKS_PER_GRAPH)
             nc.vector.quantize_mx(
                 out=codes[:].rearrange("p g e -> p (g e)").bitcast(FP8X4),
                 scales=scales[:].rearrange("p g e -> p (g e)"),
                 in_=grouped[:].rearrange("p g e t -> p (g e t)"),
             )
-
-        following = new_chunk_tiles()
-        for t in range(ROW_TILES):
-            turn_row_tile(0, t, following[0])
-        quantise_chunk(*following)
+            return codes, scales
 
         def target_terms():
-            for h in range(F_TILES // BANK_TILES):
-                target_term = psum_out.tile([P, BANK_TILES, P], F32, tag="bank")
-                for q in range(BANK_TILES):
+            for h in range(GROUPS_PER_CHUNK):
+                target_term = psum_out.tile([P, GROUP_TILES, P], F32, tag="bank")
+                for q in range(GROUP_TILES):
                     for g in range(G):
                         nc.tensor.matmul_mx(
                             out=target_term[:, q, :],
@@ -175,10 +157,10 @@ def tile_gnnlayer_pa_kernel(tc, x, e_enc, W_pre_words, W_pre_scales, b_pre, out)
                             rhs_scale=x_scales[:, g, :],
                             start=(g == 0),
                             stop=(g == G - 1),
-                            **weight(W_TARGET + g, h * BANK_TILES + q),
+                            **weight(W_TARGET + g, h * GROUP_TILES + q),
                         )
-                for q in range(BANK_TILES):
-                    ft = h * BANK_TILES + q
+                for q in range(GROUP_TILES):
+                    ft = h * GROUP_TILES + q
                     nc.scalar.activation(
                         out=base[:, ft, :],
                         in_=target_term[:, q, :],
@@ -187,111 +169,100 @@ def tile_gnnlayer_pa_kernel(tc, x, e_enc, W_pre_words, W_pre_scales, b_pre, out)
                         scale=1.0,
                     )
 
-        def aggregate(ft, b, codes, scales, stats, squares, first_target):
-            s_sum, s_min, s_max = stats[0:3]
+        def messages(b, h, codes, scales):
             moving = [(W_SOURCE + g, src_codes[:, b, g, :], src_scales[:, b, g, :]) for g in range(G)]
             moving += [(W_EDGE + g, codes[:, g, :], scales[:, g, :]) for g in range(G)]
-            bank = psum_msg.tile([P, CHUNK], F32)
-            for n, (group, rhs, rhs_scale) in enumerate(moving):
-                nc.tensor.matmul_mx(
-                    out=bank[:],
-                    rhs=rhs.bitcast(FP8X4),
-                    rhs_scale=rhs_scale,
-                    start=(n == 0),
-                    stop=(n == len(moving) - 1),
-                    **weight(group, ft),
-                )
-            s = bank[:].rearrange("p (i j) -> p i j", j=N)
+            s_group = stream.tile([P, GROUP_TILES, CHUNK], F32)
+            for q in range(GROUP_TILES):
+                bank = psum_msg.tile([P, CHUNK], F32)
+                for n, (group, rhs, rhs_scale) in enumerate(moving):
+                    nc.tensor.matmul_mx(
+                        out=bank[:],
+                        rhs=rhs.bitcast(FP8X4),
+                        rhs_scale=rhs_scale,
+                        start=(n == 0),
+                        stop=(n == len(moving) - 1),
+                        **weight(group, h * GROUP_TILES + q),
+                    )
+                nc.scalar.copy(out=s_group[:, q, :], in_=bank[:])
+            return s_group
+
+        def aggregate(s_group, h, stats, first_target):
+            s_moments, s_max, s_min = stats
+            for q in range(GROUP_TILES):
+                for pair in range(TARGETS // 2):
+                    two_targets = s_group[:, q, 2 * N * pair : 2 * N * (pair + 1)]
+                    first = MOMENTS * (first_target + 2 * pair)
+                    nc.vector.bn_stats(
+                        out=s_moments[:, h * GROUP_TILES + q, first : first + 2 * MOMENTS],
+                        in_=two_targets.rearrange("p (i j) -> p j i", j=N),
+                    )
+            s = s_group[:].rearrange("p q (i j) -> p q i j", j=N)
+            tiles = slice(h * GROUP_TILES, (h + 1) * GROUP_TILES)
             targets = slice(first_target, first_target + TARGETS)
-            nc.scalar.activation(out=squares[:, ft % SQUARE_BANKS, :, :], in_=s, func=ACT.Square)
-            nc.vector.tensor_reduce(out=s_sum[:, ft, targets], in_=s, axis=AXIS.X, op=ALU.add)
-            nc.vector.tensor_reduce(out=s_max[:, ft, targets], in_=s, axis=AXIS.X, op=ALU.max)
-            nc.vector.tensor_reduce(out=s_min[:, ft, targets], in_=s, axis=AXIS.X, op=ALU.min)
+            nc.vector.tensor_reduce(out=s_max[:, tiles, targets], in_=s, axis=AXIS.X, op=ALU.max)
+            nc.vector.tensor_reduce(out=s_min[:, tiles, targets], in_=s, axis=AXIS.X, op=ALU.min)
 
-        def add_up_squares(squares, sums):
-            width = N // 2
-            while width > 1:
-                lower = squares[:, :, :, 0:width]
-                nc.gpsimd.tensor_tensor(
-                    out=lower, in0=lower, in1=squares[:, :, :, width : 2 * width], op=ALU.add
-                )
-                width = width // 2
-            nc.gpsimd.tensor_tensor(
-                out=sums, in0=squares[:, :, :, 0], in1=squares[:, :, :, 1], op=ALU.add
-            )
-
-        def combine_graph(b, stats):
-            s_sum, s_min, s_max, s_sq = stats
-            base_b = base[:, :, b * N : (b + 1) * N]
-            result = work.tile([P, F_TILES, AGGREGATORS, N], F32)
-            s_mean = work.tile([P, F_TILES, N], F32)
-            spread = work.tile([P, F_TILES, N], F32)
+        def finish(b, h, stats):
+            s_moments, s_max, s_min = stats
+            tiles = slice(h * GROUP_TILES, (h + 1) * GROUP_TILES)
+            moments = s_moments[:, tiles, :].rearrange("p q (i m) -> p q i m", m=MOMENTS)
+            base_b = base[:, tiles, b * N : (b + 1) * N]
+            result = work.tile([P, GROUP_TILES, AGGREGATORS, N], F32)
+            spread = work.tile([P, GROUP_TILES, N], F32)
             nc.gpsimd.tensor_scalar(
-                out=s_mean[:], in0=s_sum[:], scalar1=1.0 / N, scalar2=0.0, op0=ALU.mult, op1=ALU.add
-            )
-            nc.gpsimd.tensor_tensor(out=spread[:], in0=s_sum[:], in1=s_mean[:], op=ALU.mult)
-            nc.gpsimd.tensor_tensor(out=spread[:], in0=s_sq[:], in1=spread[:], op=ALU.subtract)
-            nc.gpsimd.tensor_scalar(
-                out=spread[:], in0=spread[:], scalar1=0.0, scalar2=0.0, op0=ALU.max, op1=ALU.add
+                out=spread[:], in0=moments[:, :, :, 2], scalar1=0.0, scalar2=0.0, op0=ALU.max, op1=ALU.add
             )
             nc.scalar.activation(
                 out=result[:, :, 3, :], in_=spread[:], func=ACT.Sqrt, bias=eps[:], scale=1.0 / N
             )
-            nc.gpsimd.tensor_tensor(out=result[:, :, 0, :], in0=s_mean[:], in1=base_b, op=ALU.add)
-            nc.gpsimd.tensor_tensor(out=result[:, :, 1, :], in0=s_min[:], in1=base_b, op=ALU.add)
-            nc.gpsimd.tensor_tensor(out=result[:, :, 2, :], in0=s_max[:], in1=base_b, op=ALU.add)
-            return result
-
-        def store_graph(b, result):
-            rows = work.tile([P, F], F32)
-            for h in range(F_TILES // BANK_TILES):
-                turned = psum_out.tile([P, BANK_TILES, P], F32, tag="bank")
-                for q in range(BANK_TILES):
-                    nc.tensor.transpose(
-                        turned[:, q, :],
-                        result[:, h * BANK_TILES + q, :, :].rearrange("p a i -> p (a i)"),
-                        ident[:],
-                    )
-                nc.scalar.copy(
-                    out=rows[:, h * CHUNK : (h + 1) * CHUNK], in_=turned[:].rearrange("p q f -> p (q f)")
+            nc.gpsimd.tensor_tensor(out=result[:, :, 0, :], in0=moments[:, :, :, 1], in1=base_b, op=ALU.add)
+            nc.gpsimd.tensor_tensor(out=result[:, :, 2, :], in0=s_max[:, tiles, :], in1=base_b, op=ALU.add)
+            nc.gpsimd.tensor_tensor(out=result[:, :, 1, :], in0=s_min[:, tiles, :], in1=base_b, op=ALU.add)
+            turned = psum_out.tile([P, GROUP_TILES, P], F32, tag="bank")
+            for q in range(GROUP_TILES):
+                nc.tensor.transpose(
+                    turned[:, q, :], result[:, q, :, :].rearrange("p a i -> p (a i)"), ident[:]
                 )
+            rows = work.tile([P, CHUNK], F32)
+            nc.scalar.copy(out=rows[:], in_=turned[:].rearrange("p q f -> p (q f)"))
             for a in range(AGGREGATORS):
-                nc.sync.dma_start(out=out[b, :, a * F : (a + 1) * F], in_=rows[a * N : (a + 1) * N, :])
+                first = a * F + h * CHUNK
+                nc.sync.dma_start(out=out[b, :, first : first + CHUNK], in_=rows[a * N : (a + 1) * N, :])
 
-        stats = None
-        finished = None
-        result = None
-        squares = None
-        for c in range(CHUNKS):
-            b, part = divmod(c, CHUNKS_PER_GRAPH)
-            first_target = part * TARGETS
-            if part == 0:
-                finished = stats
-                s_sum = work.tile([P, F_TILES, N], F32)
-                s_min = work.tile([P, F_TILES, N], F32)
-                s_max = work.tile([P, F_TILES, N], F32)
-                s_sq = work.tile([P, F_TILES, N], F32)
-                stats = (s_sum, s_min, s_max, s_sq)
-            current = following
-            if c + 1 < CHUNKS:
-                following = new_chunk_tiles()
-            for ft in range(F_TILES):
-                if ft % SQUARE_BANKS == 0:
-                    squares = work.tile([P, SQUARE_BANKS, TARGETS, N], F32)
-                aggregate(ft, b, current[1], current[2], stats, squares, first_target)
-                if ft % SQUARE_BANKS == SQUARE_BANKS - 1:
-                    tiles = slice(ft + 1 - SQUARE_BANKS, ft + 1)
-                    add_up_squares(squares, stats[3][:, tiles, first_target : first_target + TARGETS])
-                if c + 1 < CHUNKS and ft < ROW_TILES:
-                    turn_row_tile(c + 1, ft, following[0])
-                if c + 1 < CHUNKS and ft == QUANTISE_BEHIND:
-                    quantise_chunk(*following)
-                if part == CHUNKS_PER_GRAPH - 1 and b + 1 < B and ft == REPEAT_BEHIND:
-                    repeat_sources(b + 1)
-                if c == 0 and ft == COMBINE_BEHIND:
+        k_onto_partitions(x_raw[:], x_grouped[:])
+        nc.vector.tensor_copy(out=bias_rows[:], in_=bias_rows_bf[:])
+        bias_turned = psum_out.tile([P, GROUP_TILES, P], F32, tag="bank")
+        nc.tensor.transpose(bias_turned[:, 0, :], bias_rows[:], ident[:])
+        nc.vector.quantize_mx(
+            out=x_codes[:].rearrange("p g r -> p (g r)").bitcast(FP8X4),
+            scales=x_scales[:].rearrange("p g r -> p (g r)"),
+            in_=x_grouped[:].rearrange("p g r t -> p (g r t)"),
+        )
+        nc.vector.tensor_copy(out=bias_col[:], in_=bias_turned[:, 0, 0:F_TILES])
+
+        following = prepare_chunk(0)
+        current = None
+        graph_stats = {}
+        for step in range(GROUPS + FINISH_LAG):
+            if step < GROUPS:
+                c, h = divmod(step, GROUPS_PER_CHUNK)
+                b, part = divmod(c, CHUNKS_PER_GRAPH)
+                if h == 0:
+                    current = following
+                if h == 0 and part == 0:
+                    s_moments = work.tile([P, F_TILES, MOMENTS * N], F32)
+                    s_max = work.tile([P, F_TILES, N], F32)
+                    s_min = work.tile([P, F_TILES, N], F32)
+                    graph_stats[b] = (s_moments, s_max, s_min)
+                s_group = messages(b, h, current[0], current[1])
+                aggregate(s_group, h, graph_stats[b], part * TARGETS)
+                if h == 0 and c + 1 < CHUNKS:
+                    following = prepare_chunk(c + 1)
+                if step == TARGET_TERMS_STEP:
                     target_terms()
-                if part == 0 and b > 0 and ft == COMBINE_BEHIND:
-                    result = combine_graph(b - 1, finished)
-                if part == 0 and b > 0 and ft == STORE_BEHIND:
-                    store_graph(b - 1, result)
-        store_graph(B - 1, combine_graph(B - 1, stats))
+            if step >= FINISH_LAG:
+                c, h = divmod(step - FINISH_LAG, GROUPS_PER_CHUNK)
+                b, part = divmod(c, CHUNKS_PER_GRAPH)
+                if part == CHUNKS_PER_GRAPH - 1:
+                    finish(b, h, graph_stats[b])

@@ -63,7 +63,7 @@ def tile_gnnlayer_pa_kernel(tc, x, e_enc, W_pre_words, W_pre_scales, b_pre, out)
         bias_rows_bf = keep.tile([P, P], BF16)
         bias_rows = keep.tile([P, P], F32)
         bias_col = keep.tile([P, F_TILES], F32)
-        base = keep.tile([P, F_TILES, B * N], F32)
+        base = keep.tile([P, F_TILES, B, AGGREGATORS, N], F32)
         eps = keep.tile([P, 1], F32)
         warm = keep.tile([P, 1], F32)
 
@@ -72,6 +72,7 @@ def tile_gnnlayer_pa_kernel(tc, x, e_enc, W_pre_words, W_pre_scales, b_pre, out)
         nc.vector.memset(bias_rows_bf[:], 0.0)
         nc.vector.memset(eps[:], EPS_STD)
         make_identity(nc, ident[:])
+        nc.gpsimd.memset(base[:, :, :, 3, :], 0.0)
         nc.scalar.activation(out=warm[:], in_=eps[:], func=ACT.Sqrt)
 
         nc.sync.dma_start(out=x_raw[:], in_=x.rearrange("b n c -> (b n) c"))
@@ -162,8 +163,11 @@ def tile_gnnlayer_pa_kernel(tc, x, e_enc, W_pre_words, W_pre_scales, b_pre, out)
                 for q in range(GROUP_TILES):
                     ft = h * GROUP_TILES + q
                     nc.scalar.activation(
-                        out=base[:, ft, :],
-                        in_=target_term[:, q, :],
+                        out=base[:, ft, :, 0:3, :],
+                        in_=target_term[:, q, :]
+                        .rearrange("p (b i) -> p b i", i=N)
+                        .unsqueeze(2)
+                        .to_broadcast([P, B, 3, N]),
                         func=ACT.Identity,
                         bias=bias_col[:, ft : ft + 1],
                         scale=1.0,
@@ -188,7 +192,7 @@ def tile_gnnlayer_pa_kernel(tc, x, e_enc, W_pre_words, W_pre_scales, b_pre, out)
             return s_group
 
         def aggregate(s_group, h, stats, first_target):
-            s_moments, s_max, s_min = stats
+            s_moments, results = stats
             for q in range(GROUP_TILES):
                 for pair in range(TARGETS // 2):
                     two_targets = s_group[:, q, 2 * N * pair : 2 * N * (pair + 1)]
@@ -200,29 +204,39 @@ def tile_gnnlayer_pa_kernel(tc, x, e_enc, W_pre_words, W_pre_scales, b_pre, out)
             s = s_group[:].rearrange("p q (i j) -> p q i j", j=N)
             tiles = slice(h * GROUP_TILES, (h + 1) * GROUP_TILES)
             targets = slice(first_target, first_target + TARGETS)
-            nc.vector.tensor_reduce(out=s_max[:, tiles, targets], in_=s, axis=AXIS.X, op=ALU.max)
-            nc.vector.tensor_reduce(out=s_min[:, tiles, targets], in_=s, axis=AXIS.X, op=ALU.min)
+            nc.vector.tensor_reduce(out=results[:, tiles, 2, targets], in_=s, axis=AXIS.X, op=ALU.max)
+            nc.vector.tensor_reduce(out=results[:, tiles, 1, targets], in_=s, axis=AXIS.X, op=ALU.min)
 
         def finish(b, h, stats):
-            s_moments, s_max, s_min = stats
+            s_moments, results = stats
             tiles = slice(h * GROUP_TILES, (h + 1) * GROUP_TILES)
             moments = s_moments[:, tiles, :].rearrange("p q (i m) -> p q i m", m=MOMENTS)
-            base_b = base[:, tiles, b * N : (b + 1) * N]
-            result = work.tile([P, GROUP_TILES, AGGREGATORS, N], F32)
             spread = work.tile([P, GROUP_TILES, N], F32)
             nc.gpsimd.tensor_scalar(
                 out=spread[:], in0=moments[:, :, :, 2], scalar1=0.0, scalar2=0.0, op0=ALU.max, op1=ALU.add
             )
             nc.scalar.activation(
-                out=result[:, :, 3, :], in_=spread[:], func=ACT.Sqrt, bias=eps[:], scale=1.0 / N
+                out=results[:, tiles, 3, :], in_=spread[:], func=ACT.Sqrt, bias=eps[:], scale=1.0 / N
             )
-            nc.gpsimd.tensor_tensor(out=result[:, :, 0, :], in0=moments[:, :, :, 1], in1=base_b, op=ALU.add)
-            nc.gpsimd.tensor_tensor(out=result[:, :, 2, :], in0=s_max[:, tiles, :], in1=base_b, op=ALU.add)
-            nc.gpsimd.tensor_tensor(out=result[:, :, 1, :], in0=s_min[:, tiles, :], in1=base_b, op=ALU.add)
+            nc.gpsimd.tensor_copy(out=results[:, tiles, 0, :], in_=moments[:, :, :, 1])
             turned = psum_out.tile([P, GROUP_TILES, P], F32, tag="bank")
             for q in range(GROUP_TILES):
-                nc.tensor.transpose(
-                    turned[:, q, :], result[:, q, :, :].rearrange("p a i -> p (a i)"), ident[:]
+                ft = h * GROUP_TILES + q
+                nc.tensor.matmul(
+                    turned[:, q, :],
+                    lhsT=results[:, ft, :, :].rearrange("p a i -> p (a i)"),
+                    rhs=ident[:],
+                    is_transpose=True,
+                    start=True,
+                    stop=False,
+                )
+                nc.tensor.matmul(
+                    turned[:, q, :],
+                    lhsT=base[:, ft, b, :, :].rearrange("p a i -> p (a i)"),
+                    rhs=ident[:],
+                    is_transpose=True,
+                    start=False,
+                    stop=True,
                 )
             rows = work.tile([P, CHUNK], F32)
             nc.scalar.copy(out=rows[:], in_=turned[:].rearrange("p q f -> p (q f)"))
@@ -252,9 +266,8 @@ def tile_gnnlayer_pa_kernel(tc, x, e_enc, W_pre_words, W_pre_scales, b_pre, out)
                     current = following
                 if h == 0 and part == 0:
                     s_moments = work.tile([P, F_TILES, MOMENTS * N], F32)
-                    s_max = work.tile([P, F_TILES, N], F32)
-                    s_min = work.tile([P, F_TILES, N], F32)
-                    graph_stats[b] = (s_moments, s_max, s_min)
+                    results = work.tile([P, F_TILES, AGGREGATORS, N], F32)
+                    graph_stats[b] = (s_moments, results)
                 s_group = messages(b, h, current[0], current[1])
                 aggregate(s_group, h, graph_stats[b], part * TARGETS)
                 if h == 0 and c + 1 < CHUNKS:

@@ -34,6 +34,9 @@ GROUPS_PER_CHUNK = F_TILES // GROUP_TILES
 GROUPS = CHUNKS * GROUPS_PER_CHUNK
 MOMENTS = 3
 FINISH_LAG = 2
+SHARED_TILES = (1, 3)
+SHARE_LAG = 2
+HALF = N // 2
 TARGET_TERMS_STEP = 1
 
 FLOPS = 2 * (B * N * N + 2 * B * N) * C * F
@@ -41,14 +44,14 @@ FLOPS = 2 * (B * N * N + 2 * B * N) * C * F
 
 def tile_gnnlayer_pa_kernel(tc, x, e_enc, W_pre_words, W_pre_scales, b_pre, out):
     nc = tc.nc
+    SHARED_ROWS = len(SHARED_TILES) * TARGETS
     with ExitStack() as ctx:
         ctx.enter_context(tc.manual_schedule())
         keep = ctx.enter_context(tc.tile_pool(name="keep", bufs=1))
         work = ctx.enter_context(tc.tile_pool(name="work", bufs=2))
         stream = ctx.enter_context(tc.tile_pool(name="stream", bufs=3))
-        psum_turn = ctx.enter_context(tc.psum_pool(name="psum_turn", bufs=2))
         psum_msg = ctx.enter_context(tc.psum_pool(name="psum_msg", bufs=4))
-        psum_out = ctx.enter_context(tc.psum_pool(name="psum_out", bufs=2))
+        psum_aux = ctx.enter_context(tc.psum_pool(name="psum_aux", bufs=4))
 
         x_raw = keep.tile([P, C], BF16)
         e_raw = keep.tile([P, CHUNKS, ROW_TILES, C], BF16)
@@ -107,7 +110,7 @@ def tile_gnnlayer_pa_kernel(tc, x, e_enc, W_pre_words, W_pre_scales, b_pre, out)
 
         def k_onto_partitions(rows_bf16, grouped):
             words = rows_bf16.bitcast(F32)
-            turned = psum_turn.tile([P, G, 2, P], F32)
+            turned = psum_aux.tile([P, G, 2, P], F32, tag="bank")
             for g in range(G):
                 for u in range(2):
                     nc.tensor.transpose(
@@ -149,7 +152,7 @@ def tile_gnnlayer_pa_kernel(tc, x, e_enc, W_pre_words, W_pre_scales, b_pre, out)
 
         def target_terms():
             for h in range(GROUPS_PER_CHUNK):
-                target_term = psum_out.tile([P, GROUP_TILES, P], F32, tag="bank")
+                target_term = psum_aux.tile([P, GROUP_TILES, P], F32, tag="bank")
                 for q in range(GROUP_TILES):
                     for g in range(G):
                         nc.tensor.matmul_mx(
@@ -173,10 +176,13 @@ def tile_gnnlayer_pa_kernel(tc, x, e_enc, W_pre_words, W_pre_scales, b_pre, out)
                         scale=1.0,
                     )
 
-        def messages(b, h, codes, scales):
+        def messages(b, h, codes, scales, shared):
             moving = [(W_SOURCE + g, src_codes[:, b, g, :], src_scales[:, b, g, :]) for g in range(G)]
             moving += [(W_EDGE + g, codes[:, g, :], scales[:, g, :]) for g in range(G)]
-            s_group = stream.tile([P, GROUP_TILES, CHUNK], F32)
+            banks = []
+            copies = None
+            if shared:
+                copies = stream.tile([P, SHARED_ROWS, N], F32)
             for q in range(GROUP_TILES):
                 bank = psum_msg.tile([P, CHUNK], F32)
                 for n, (group, rhs, rhs_scale) in enumerate(moving):
@@ -188,38 +194,80 @@ def tile_gnnlayer_pa_kernel(tc, x, e_enc, W_pre_words, W_pre_scales, b_pre, out)
                         stop=(n == len(moving) - 1),
                         **weight(group, h * GROUP_TILES + q),
                     )
-                nc.scalar.copy(out=s_group[:, q, :], in_=bank[:])
-            return s_group
+                if shared and q in SHARED_TILES:
+                    slot = SHARED_TILES.index(q)
+                    nc.scalar.copy(
+                        out=copies[:, slot * TARGETS : (slot + 1) * TARGETS, :].rearrange("p i j -> p (i j)"),
+                        in_=bank[:],
+                    )
+                banks.append(bank)
+            return banks, copies
 
-        def aggregate(s_group, h, stats, first_target):
+        def differences(copies):
+            apart = stream.tile([P, SHARED_ROWS, HALF], F32)
+            nc.gpsimd.tensor_tensor(
+                out=apart[:], in0=copies[:, :, HALF:N], in1=copies[:, :, 0:HALF], op=ALU.subtract
+            )
+            return apart
+
+        def clip(apart):
+            clipped = stream.tile([P, SHARED_ROWS, 2, HALF], F32)
+            below = stream.tile([P, SHARED_ROWS, HALF], F32)
+            nc.scalar.activation(out=clipped[:, :, 0, :], in_=apart[:], func=ACT.Relu)
+            nc.scalar.activation(out=below[:], in_=apart[:], func=ACT.Relu, scale=-1.0)
+            nc.scalar.activation(out=clipped[:, :, 1, :], in_=below[:], func=ACT.Copy, scale=-1.0)
+            return clipped
+
+        def larger_and_smaller(copies, clipped):
+            sorted_pairs = stream.tile([P, SHARED_ROWS, 2, HALF], F32)
+            nc.gpsimd.tensor_tensor(
+                out=sorted_pairs[:],
+                in0=copies[:, :, 0:HALF].unsqueeze(2).to_broadcast([P, SHARED_ROWS, 2, HALF]),
+                in1=clipped[:],
+                op=ALU.add,
+            )
+            return sorted_pairs
+
+        def shared_extremes(sorted_pairs, h, stats, first_target):
+            results = stats[1]
+            first = h * GROUP_TILES + SHARED_TILES[0]
+            last = h * GROUP_TILES + SHARED_TILES[-1]
+            tiles = slice(first, last + 1, max(1, last - first))
+            targets = slice(first_target, first_target + TARGETS)
+            pairs = sorted_pairs[:].rearrange("p (n i) m k -> p n i m k", i=TARGETS)
+            nc.vector.tensor_reduce(out=results[:, tiles, 2, targets], in_=pairs[:, :, :, 0, :], axis=AXIS.X, op=ALU.max)
+            nc.vector.tensor_reduce(out=results[:, tiles, 1, targets], in_=pairs[:, :, :, 1, :], axis=AXIS.X, op=ALU.min)
+
+        def aggregate(banks, h, stats, first_target, shared):
             s_moments, results = stats
+            targets = slice(first_target, first_target + TARGETS)
             for q in range(GROUP_TILES):
+                ft = h * GROUP_TILES + q
                 for pair in range(TARGETS // 2):
-                    two_targets = s_group[:, q, 2 * N * pair : 2 * N * (pair + 1)]
+                    two_targets = banks[q][:, 2 * N * pair : 2 * N * (pair + 1)]
                     first = MOMENTS * (first_target + 2 * pair)
                     nc.vector.bn_stats(
-                        out=s_moments[:, h * GROUP_TILES + q, first : first + 2 * MOMENTS],
+                        out=s_moments[:, ft, first : first + 2 * MOMENTS],
                         in_=two_targets.rearrange("p (i j) -> p j i", j=N),
                     )
-            s = s_group[:].rearrange("p q (i j) -> p q i j", j=N)
-            tiles = slice(h * GROUP_TILES, (h + 1) * GROUP_TILES)
-            targets = slice(first_target, first_target + TARGETS)
-            nc.vector.tensor_reduce(out=results[:, tiles, 2, targets], in_=s, axis=AXIS.X, op=ALU.max)
-            nc.vector.tensor_reduce(out=results[:, tiles, 1, targets], in_=s, axis=AXIS.X, op=ALU.min)
+                if shared and q in SHARED_TILES:
+                    continue
+                s = banks[q][:].rearrange("p (i j) -> p i j", j=N)
+                nc.vector.tensor_reduce(out=results[:, ft, 2, targets], in_=s, axis=AXIS.X, op=ALU.max)
+                nc.vector.tensor_reduce(out=results[:, ft, 1, targets], in_=s, axis=AXIS.X, op=ALU.min)
 
-        def finish(b, h, stats):
+        def finish_moments(b, h, stats):
             s_moments, results = stats
             tiles = slice(h * GROUP_TILES, (h + 1) * GROUP_TILES)
             moments = s_moments[:, tiles, :].rearrange("p q (i m) -> p q i m", m=MOMENTS)
-            spread = work.tile([P, GROUP_TILES, N], F32)
-            nc.gpsimd.tensor_scalar(
-                out=spread[:], in0=moments[:, :, :, 2], scalar1=0.0, scalar2=0.0, op0=ALU.max, op1=ALU.add
-            )
-            nc.scalar.activation(
-                out=results[:, tiles, 3, :], in_=spread[:], func=ACT.Sqrt, bias=eps[:], scale=1.0 / N
-            )
-            nc.gpsimd.tensor_copy(out=results[:, tiles, 0, :], in_=moments[:, :, :, 1])
-            turned = psum_out.tile([P, GROUP_TILES, P], F32, tag="bank")
+            variance = work.tile([P, GROUP_TILES, N], F32)
+            nc.scalar.activation(out=variance[:], in_=moments[:, :, :, 2], func=ACT.Relu, scale=1.0 / N)
+            nc.scalar.activation(out=results[:, tiles, 3, :], in_=variance[:], func=ACT.Sqrt, bias=eps[:])
+            nc.scalar.copy(out=results[:, tiles, 0, :], in_=moments[:, :, :, 1])
+
+        def finish_store(b, h, stats):
+            results = stats[1]
+            turned = psum_aux.tile([P, GROUP_TILES, P], F32, tag="bank")
             for q in range(GROUP_TILES):
                 ft = h * GROUP_TILES + q
                 nc.tensor.matmul(
@@ -246,7 +294,7 @@ def tile_gnnlayer_pa_kernel(tc, x, e_enc, W_pre_words, W_pre_scales, b_pre, out)
 
         k_onto_partitions(x_raw[:], x_grouped[:])
         nc.vector.tensor_copy(out=bias_rows[:], in_=bias_rows_bf[:])
-        bias_turned = psum_out.tile([P, GROUP_TILES, P], F32, tag="bank")
+        bias_turned = psum_aux.tile([P, GROUP_TILES, P], F32, tag="bank")
         nc.tensor.transpose(bias_turned[:, 0, :], bias_rows[:], ident[:])
         nc.vector.quantize_mx(
             out=x_codes[:].rearrange("p g r -> p (g r)").bitcast(FP8X4),
@@ -258,7 +306,8 @@ def tile_gnnlayer_pa_kernel(tc, x, e_enc, W_pre_words, W_pre_scales, b_pre, out)
         following = prepare_chunk(0)
         current = None
         graph_stats = {}
-        for step in range(GROUPS + FINISH_LAG):
+        in_flight = {}
+        for step in range(GROUPS + 1):
             if step < GROUPS:
                 c, h = divmod(step, GROUPS_PER_CHUNK)
                 b, part = divmod(c, CHUNKS_PER_GRAPH)
@@ -268,14 +317,31 @@ def tile_gnnlayer_pa_kernel(tc, x, e_enc, W_pre_words, W_pre_scales, b_pre, out)
                     s_moments = work.tile([P, F_TILES, MOMENTS * N], F32)
                     results = work.tile([P, F_TILES, AGGREGATORS, N], F32)
                     graph_stats[b] = (s_moments, results)
-                s_group = messages(b, h, current[0], current[1])
-                aggregate(s_group, h, graph_stats[b], part * TARGETS)
+                shared = step < GROUPS - 3
+                if step - 1 in in_flight:
+                    in_flight[step - 1].append(clip(in_flight[step - 1][1]))
+                banks, copies = messages(b, h, current[0], current[1], shared)
+                if step - SHARE_LAG in in_flight:
+                    earlier = in_flight[step - SHARE_LAG]
+                    earlier.append(larger_and_smaller(earlier[0], earlier[2]))
+                if shared:
+                    in_flight[step] = [copies, differences(copies)]
+                aggregate(banks, h, graph_stats[b], part * TARGETS, shared)
                 if h == 0 and c + 1 < CHUNKS:
                     following = prepare_chunk(c + 1)
                 if step == TARGET_TERMS_STEP:
                     target_terms()
-            if step >= FINISH_LAG:
-                c, h = divmod(step - FINISH_LAG, GROUPS_PER_CHUNK)
+            if step - SHARE_LAG in in_flight:
+                c, h = divmod(step - SHARE_LAG, GROUPS_PER_CHUNK)
                 b, part = divmod(c, CHUNKS_PER_GRAPH)
-                if part == CHUNKS_PER_GRAPH - 1:
-                    finish(b, h, graph_stats[b])
+                shared_extremes(in_flight[step - SHARE_LAG][3], h, graph_stats[b], part * TARGETS)
+            for done in range(step + 1):
+                c, h = divmod(done, GROUPS_PER_CHUNK)
+                b, part = divmod(c, CHUNKS_PER_GRAPH)
+                if part != CHUNKS_PER_GRAPH - 1:
+                    continue
+                latest = max(GROUPS - 1, done + 1)
+                if min(done + FINISH_LAG, latest) == step:
+                    finish_moments(b, h, graph_stats[b])
+                if min(done + FINISH_LAG + 1, latest) == step:
+                    finish_store(b, h, graph_stats[b])

@@ -34,7 +34,7 @@ GROUPS_PER_CHUNK = F_TILES // GROUP_TILES
 GROUPS = CHUNKS * GROUPS_PER_CHUNK
 MOMENTS = 3
 FINISH_LAG = 2
-SHARED_TILES = (1, 3)
+SHARED_TILES = (1, 2, 3)
 SHARE_LAG = 2
 HALF = N // 2
 TARGET_TERMS_STEP = 1
@@ -50,6 +50,7 @@ def tile_gnnlayer_pa_kernel(tc, x, e_enc, W_pre_words, W_pre_scales, b_pre, out)
         keep = ctx.enter_context(tc.tile_pool(name="keep", bufs=1))
         work = ctx.enter_context(tc.tile_pool(name="work", bufs=2))
         stream = ctx.enter_context(tc.tile_pool(name="stream", bufs=3))
+        stage = ctx.enter_context(tc.tile_pool(name="stage", bufs=2))
         psum_msg = ctx.enter_context(tc.psum_pool(name="psum_msg", bufs=4))
         psum_aux = ctx.enter_context(tc.psum_pool(name="psum_aux", bufs=4))
 
@@ -204,27 +205,24 @@ def tile_gnnlayer_pa_kernel(tc, x, e_enc, W_pre_words, W_pre_scales, b_pre, out)
             return banks, copies
 
         def differences(copies):
-            apart = stream.tile([P, SHARED_ROWS, HALF], F32)
+            apart = stage.tile([P, SHARED_ROWS, HALF], F32)
             nc.gpsimd.tensor_tensor(
                 out=apart[:], in0=copies[:, :, HALF:N], in1=copies[:, :, 0:HALF], op=ALU.subtract
             )
             return apart
 
         def clip(apart):
-            clipped = stream.tile([P, SHARED_ROWS, 2, HALF], F32)
-            below = stream.tile([P, SHARED_ROWS, HALF], F32)
-            nc.scalar.activation(out=clipped[:, :, 0, :], in_=apart[:], func=ACT.Relu)
-            nc.scalar.activation(out=below[:], in_=apart[:], func=ACT.Relu, scale=-1.0)
-            nc.scalar.activation(out=clipped[:, :, 1, :], in_=below[:], func=ACT.Copy, scale=-1.0)
+            clipped = stage.tile([P, SHARED_ROWS, HALF], F32)
+            nc.scalar.activation(out=clipped[:], in_=apart[:], func=ACT.Relu)
             return clipped
 
         def larger_and_smaller(copies, clipped):
-            sorted_pairs = stream.tile([P, SHARED_ROWS, 2, HALF], F32)
+            sorted_pairs = stage.tile([P, SHARED_ROWS, 2, HALF], F32)
             nc.gpsimd.tensor_tensor(
-                out=sorted_pairs[:],
-                in0=copies[:, :, 0:HALF].unsqueeze(2).to_broadcast([P, SHARED_ROWS, 2, HALF]),
-                in1=clipped[:],
-                op=ALU.add,
+                out=sorted_pairs[:, :, 0, :], in0=copies[:, :, 0:HALF], in1=clipped[:], op=ALU.add
+            )
+            nc.gpsimd.tensor_tensor(
+                out=sorted_pairs[:, :, 1, :], in0=copies[:, :, HALF:N], in1=clipped[:], op=ALU.subtract
             )
             return sorted_pairs
 
@@ -232,29 +230,31 @@ def tile_gnnlayer_pa_kernel(tc, x, e_enc, W_pre_words, W_pre_scales, b_pre, out)
             results = stats[1]
             first = h * GROUP_TILES + SHARED_TILES[0]
             last = h * GROUP_TILES + SHARED_TILES[-1]
-            tiles = slice(first, last + 1, max(1, last - first))
+            tiles = slice(first, last + 1, SHARED_TILES[1] - SHARED_TILES[0])
             targets = slice(first_target, first_target + TARGETS)
             pairs = sorted_pairs[:].rearrange("p (n i) m k -> p n i m k", i=TARGETS)
             nc.vector.tensor_reduce(out=results[:, tiles, 2, targets], in_=pairs[:, :, :, 0, :], axis=AXIS.X, op=ALU.max)
             nc.vector.tensor_reduce(out=results[:, tiles, 1, targets], in_=pairs[:, :, :, 1, :], axis=AXIS.X, op=ALU.min)
 
-        def aggregate(banks, h, stats, first_target, shared):
+        def aggregate(banks, copies, h, stats, first_target, moments=True, extremes=True):
             s_moments, results = stats
             targets = slice(first_target, first_target + TARGETS)
             for q in range(GROUP_TILES):
                 ft = h * GROUP_TILES + q
-                for pair in range(TARGETS // 2):
-                    two_targets = banks[q][:, 2 * N * pair : 2 * N * (pair + 1)]
+                s = banks[q][:].rearrange("p (i j) -> p i j", j=N)
+                shared = copies is not None and q in SHARED_TILES
+                if shared:
+                    slot = SHARED_TILES.index(q)
+                    s = copies[:, slot * TARGETS : (slot + 1) * TARGETS, :]
+                for pair in range(TARGETS // 2 if moments else 0):
                     first = MOMENTS * (first_target + 2 * pair)
                     nc.vector.bn_stats(
                         out=s_moments[:, ft, first : first + 2 * MOMENTS],
-                        in_=two_targets.rearrange("p (i j) -> p j i", j=N),
+                        in_=s[:, 2 * pair : 2 * pair + 2, :].rearrange("p i j -> p j i"),
                     )
-                if shared and q in SHARED_TILES:
-                    continue
-                s = banks[q][:].rearrange("p (i j) -> p i j", j=N)
-                nc.vector.tensor_reduce(out=results[:, ft, 2, targets], in_=s, axis=AXIS.X, op=ALU.max)
-                nc.vector.tensor_reduce(out=results[:, ft, 1, targets], in_=s, axis=AXIS.X, op=ALU.min)
+                if extremes and not shared:
+                    nc.vector.tensor_reduce(out=results[:, ft, 2, targets], in_=s, axis=AXIS.X, op=ALU.max)
+                    nc.vector.tensor_reduce(out=results[:, ft, 1, targets], in_=s, axis=AXIS.X, op=ALU.min)
 
         def finish_moments(b, h, stats):
             s_moments, results = stats
@@ -307,41 +307,46 @@ def tile_gnnlayer_pa_kernel(tc, x, e_enc, W_pre_words, W_pre_scales, b_pre, out)
         current = None
         graph_stats = {}
         in_flight = {}
-        for step in range(GROUPS + 1):
-            if step < GROUPS:
-                c, h = divmod(step, GROUPS_PER_CHUNK)
-                b, part = divmod(c, CHUNKS_PER_GRAPH)
-                if h == 0:
-                    current = following
-                if h == 0 and part == 0:
-                    s_moments = work.tile([P, F_TILES, MOMENTS * N], F32)
-                    results = work.tile([P, F_TILES, AGGREGATORS, N], F32)
-                    graph_stats[b] = (s_moments, results)
-                shared = step < GROUPS - 3
-                if step - 1 in in_flight:
-                    in_flight[step - 1].append(clip(in_flight[step - 1][1]))
-                banks, copies = messages(b, h, current[0], current[1], shared)
-                if step - SHARE_LAG in in_flight:
-                    earlier = in_flight[step - SHARE_LAG]
-                    earlier.append(larger_and_smaller(earlier[0], earlier[2]))
-                if shared:
-                    in_flight[step] = [copies, differences(copies)]
-                aggregate(banks, h, graph_stats[b], part * TARGETS, shared)
-                if h == 0 and c + 1 < CHUNKS:
-                    following = prepare_chunk(c + 1)
-                if step == TARGET_TERMS_STEP:
-                    target_terms()
+        for step in range(GROUPS):
+            c, h = divmod(step, GROUPS_PER_CHUNK)
+            b, part = divmod(c, CHUNKS_PER_GRAPH)
+            if h == 0:
+                current = following
+            if h == 0 and part == 0:
+                s_moments = work.tile([P, F_TILES, MOMENTS * N], F32)
+                results = work.tile([P, F_TILES, AGGREGATORS, N], F32)
+                graph_stats[b] = (s_moments, results)
+            stats = graph_stats[b]
+            shared = step < GROUPS - 3
+            if step - 1 in in_flight:
+                in_flight[step - 1].append(clip(in_flight[step - 1][1]))
+            banks, copies = messages(b, h, current[0], current[1], shared)
+            if step - SHARE_LAG in in_flight:
+                earlier = in_flight[step - SHARE_LAG]
+                earlier.append(larger_and_smaller(earlier[0], earlier[2]))
+            if shared:
+                in_flight[step] = [copies, differences(copies)]
+            if step < GROUPS - 1:
+                aggregate(banks, copies, h, stats, part * TARGETS)
+            else:
+                finish_moments(b, h - 1, stats)
+                finish_store(b, h - 1, stats)
+                aggregate(banks, copies, h, stats, part * TARGETS, extremes=False)
+                finish_moments(b, h, stats)
+                aggregate(banks, copies, h, stats, part * TARGETS, moments=False)
+                finish_store(b, h, stats)
+            if h == 0 and c + 1 < CHUNKS:
+                following = prepare_chunk(c + 1)
+            if step == TARGET_TERMS_STEP:
+                target_terms()
             if step - SHARE_LAG in in_flight:
                 c, h = divmod(step - SHARE_LAG, GROUPS_PER_CHUNK)
                 b, part = divmod(c, CHUNKS_PER_GRAPH)
                 shared_extremes(in_flight[step - SHARE_LAG][3], h, graph_stats[b], part * TARGETS)
-            for done in range(step + 1):
+            for done in range(GROUPS - GROUPS_PER_CHUNK):
                 c, h = divmod(done, GROUPS_PER_CHUNK)
                 b, part = divmod(c, CHUNKS_PER_GRAPH)
-                if part != CHUNKS_PER_GRAPH - 1:
-                    continue
-                latest = max(GROUPS - 1, done + 1)
-                if min(done + FINISH_LAG, latest) == step:
+                if part == CHUNKS_PER_GRAPH - 1 and done + FINISH_LAG == step:
                     finish_moments(b, h, graph_stats[b])
-                if min(done + FINISH_LAG + 1, latest) == step:
+                if part == CHUNKS_PER_GRAPH - 1 and done + FINISH_LAG + 1 == step:
                     finish_store(b, h, graph_stats[b])

@@ -136,14 +136,15 @@ def tile_gnnlayer_pa_kernel(tc, x, e_enc, W_pre_words, W_pre_scales, b_pre, out)
                 in_=x_scales[:, :, nodes].bitcast(I32).unsqueeze(2).to_broadcast([P, G, TARGETS, N // 4]),
             )
 
-        def prepare_chunk(c):
+        def turn_chunk(c):
             grouped = work.tile([P, G, CHUNK, PACK], BF16, align_bytes=64)
-            codes = work.tile([P, G, CHUNK], U32, align_bytes=64)
-            scales = work.tile([P, G, CHUNK], U8, align_bytes=64)
             for t in range(ROW_TILES):
                 k_onto_partitions(e_raw[:, c, t, :], grouped[:, :, t * P : (t + 1) * P, :])
-            if c % CHUNKS_PER_GRAPH == 0:
-                repeat_sources(c // CHUNKS_PER_GRAPH)
+            return grouped
+
+        def quantise_chunk(grouped):
+            codes = work.tile([P, G, CHUNK], U32, align_bytes=64)
+            scales = work.tile([P, G, CHUNK], U8, align_bytes=64)
             nc.vector.quantize_mx(
                 out=codes[:].rearrange("p g e -> p (g e)").bitcast(FP8X4),
                 scales=scales[:].rearrange("p g e -> p (g e)"),
@@ -236,9 +237,10 @@ def tile_gnnlayer_pa_kernel(tc, x, e_enc, W_pre_words, W_pre_scales, b_pre, out)
             nc.vector.tensor_reduce(out=results[:, tiles, 2, targets], in_=pairs[:, :, :, 0, :], axis=AXIS.X, op=ALU.max)
             nc.vector.tensor_reduce(out=results[:, tiles, 1, targets], in_=pairs[:, :, :, 1, :], axis=AXIS.X, op=ALU.min)
 
-        def aggregate(banks, copies, h, stats, first_target, moments=True, extremes=True):
+        def aggregate(banks, copies, h, stats, first_target, moments=True, extremes=True, turned_chunk=None):
             s_moments, results = stats
             targets = slice(first_target, first_target + TARGETS)
+            quantised = None
             for q in range(GROUP_TILES):
                 ft = h * GROUP_TILES + q
                 s = banks[q][:].rearrange("p (i j) -> p i j", j=N)
@@ -255,6 +257,9 @@ def tile_gnnlayer_pa_kernel(tc, x, e_enc, W_pre_words, W_pre_scales, b_pre, out)
                 if extremes and not shared:
                     nc.vector.tensor_reduce(out=results[:, ft, 2, targets], in_=s, axis=AXIS.X, op=ALU.max)
                     nc.vector.tensor_reduce(out=results[:, ft, 1, targets], in_=s, axis=AXIS.X, op=ALU.min)
+                if q == 0 and turned_chunk is not None:
+                    quantised = quantise_chunk(turned_chunk)
+            return quantised
 
         def finish_moments(b, h, stats):
             s_moments, results = stats
@@ -303,7 +308,11 @@ def tile_gnnlayer_pa_kernel(tc, x, e_enc, W_pre_words, W_pre_scales, b_pre, out)
         )
         nc.vector.tensor_copy(out=bias_col[:], in_=bias_turned[:, 0, 0:F_TILES])
 
-        following = prepare_chunk(0)
+        for b in range(B):
+            repeat_sources(b)
+
+        following = quantise_chunk(turn_chunk(0))
+        turned_chunk = None
         current = None
         graph_stats = {}
         in_flight = {}
@@ -327,7 +336,10 @@ def tile_gnnlayer_pa_kernel(tc, x, e_enc, W_pre_words, W_pre_scales, b_pre, out)
             if shared:
                 in_flight[step] = [copies, differences(copies)]
             if step < GROUPS - 1:
-                aggregate(banks, copies, h, stats, part * TARGETS)
+                quantised = aggregate(banks, copies, h, stats, part * TARGETS, turned_chunk=turned_chunk)
+                if quantised is not None:
+                    following = quantised
+                    turned_chunk = None
             else:
                 finish_moments(b, h - 1, stats)
                 finish_store(b, h - 1, stats)
@@ -336,7 +348,7 @@ def tile_gnnlayer_pa_kernel(tc, x, e_enc, W_pre_words, W_pre_scales, b_pre, out)
                 aggregate(banks, copies, h, stats, part * TARGETS, moments=False)
                 finish_store(b, h, stats)
             if h == 0 and c + 1 < CHUNKS:
-                following = prepare_chunk(c + 1)
+                turned_chunk = turn_chunk(c + 1)
             if step == TARGET_TERMS_STEP:
                 target_terms()
             if step - SHARE_LAG in in_flight:

@@ -257,7 +257,7 @@ def tile_gnnlayer_pa_kernel(tc, x, e_enc, W_pre_words, W_pre_scales, b_pre, out)
                 if extremes and not shared:
                     nc.vector.tensor_reduce(out=results[:, ft, 2, targets], in_=s, axis=AXIS.X, op=ALU.max)
                     nc.vector.tensor_reduce(out=results[:, ft, 1, targets], in_=s, axis=AXIS.X, op=ALU.min)
-                if q == 0 and turned_chunk is not None:
+                if q == 1 and turned_chunk is not None:
                     quantised = quantise_chunk(turned_chunk)
             return quantised
 
@@ -326,7 +326,7 @@ def tile_gnnlayer_pa_kernel(tc, x, e_enc, W_pre_words, W_pre_scales, b_pre, out)
                 results = work.tile([P, F_TILES, AGGREGATORS, N], F32)
                 graph_stats[b] = (s_moments, results)
             stats = graph_stats[b]
-            shared = step < GROUPS - 3
+            shared = step < GROUPS - SHARE_LAG
             if step - 1 in in_flight:
                 in_flight[step - 1].append(clip(in_flight[step - 1][1]))
             banks, copies = messages(b, h, current[0], current[1], shared)
@@ -346,12 +346,13 @@ def tile_gnnlayer_pa_kernel(tc, x, e_enc, W_pre_words, W_pre_scales, b_pre, out)
                 aggregate(banks, copies, h, stats, part * TARGETS, extremes=False)
                 finish_moments(b, h, stats)
                 aggregate(banks, copies, h, stats, part * TARGETS, moments=False)
+                shared_extremes(in_flight[step - SHARE_LAG][3], h, stats, 0)
                 finish_store(b, h, stats)
             if h == 0 and c + 1 < CHUNKS:
                 turned_chunk = turn_chunk(c + 1)
             if step == TARGET_TERMS_STEP:
                 target_terms()
-            if step - SHARE_LAG in in_flight:
+            if step - SHARE_LAG in in_flight and step < GROUPS - 1:
                 c, h = divmod(step - SHARE_LAG, GROUPS_PER_CHUNK)
                 b, part = divmod(c, CHUNKS_PER_GRAPH)
                 shared_extremes(in_flight[step - SHARE_LAG][3], h, graph_stats[b], part * TARGETS)

@@ -56,8 +56,8 @@ def tile_gnnlayer_pa_kernel(tc, x, e_enc, W_pre_words, W_pre_scales, b_pre, out)
 
         x_raw = keep.tile([P, C], BF16)
         e_raw = keep.tile([P, CHUNKS, ROW_TILES, C], BF16)
-        w_words = keep.tile([P, 3 * G, 2 * F], U8, align_bytes=64)
-        w_scales = keep.tile([P, 3 * G, F], U8, align_bytes=64)
+        w_words = [keep.tile([P, 3 * G, F], U8, align_bytes=64, name="w_words_%d" % h) for h in range(2)]
+        w_scales = [keep.tile([P, 3 * G, F // 2], U8, align_bytes=64, name="w_scales_%d" % h) for h in range(2)]
         x_grouped = keep.tile([P, G, P, PACK], BF16, align_bytes=64)
         x_codes = keep.tile([P, G, P], U32, align_bytes=64)
         x_scales = keep.tile([P, G, P], U8, align_bytes=64)
@@ -71,7 +71,8 @@ def tile_gnnlayer_pa_kernel(tc, x, e_enc, W_pre_words, W_pre_scales, b_pre, out)
         eps = keep.tile([P, 1], F32)
         warm = keep.tile([P, 1], F32)
 
-        nc.vector.memset(w_scales[:].bitcast(I32), 0)
+        for h in range(2):
+            nc.vector.memset(w_scales[h][:].bitcast(I32), 0)
         nc.vector.memset(x_scales[:].bitcast(I32), 0)
         nc.vector.memset(bias_rows_bf[:], 0.0)
         nc.vector.memset(eps[:], EPS_STD)
@@ -80,7 +81,6 @@ def tile_gnnlayer_pa_kernel(tc, x, e_enc, W_pre_words, W_pre_scales, b_pre, out)
         nc.scalar.activation(out=warm[:], in_=eps[:], func=ACT.Sqrt)
 
         nc.sync.dma_start(out=x_raw[:], in_=x.rearrange("b n c -> (b n) c"))
-        nc.sync.dma_start(out=bias_rows_bf[0:F_TILES, :], in_=b_pre.rearrange("(t f) -> t f", f=P))
         edges = e_enc.rearrange("b i j c -> (b i j) c")
 
         def load_chunk(c):
@@ -88,24 +88,33 @@ def tile_gnnlayer_pa_kernel(tc, x, e_enc, W_pre_words, W_pre_scales, b_pre, out)
                 first_row = c * CHUNK + t * P
                 nc.sync.dma_start(out=e_raw[:, c, t, :], in_=edges[first_row : first_row + P, :])
 
-        def load_weights(first_group, groups):
+        def load_weights(first_group, groups, h):
             chosen = slice(first_group, first_group + groups)
             nc.sync.dma_start(
-                out=w_words[:, chosen, :].bitcast(I32),
-                in_=W_pre_words[chosen].rearrange("g p n -> p g n").bitcast(I32),
+                out=w_words[h][:, chosen, :].bitcast(I32),
+                in_=W_pre_words[chosen].rearrange("g p n -> p g n")[:, :, h * F : (h + 1) * F].bitcast(I32),
             )
 
-        load_chunk(0)
-        scale_rows = W_pre_scales.rearrange("g (h m r) n -> m r h g n", h=2, m=2, r=4)
-        for m in range(2):
+        scale_rows = W_pre_scales.rearrange("g (m r) n -> r m g n", r=4)
+
+        def load_scales(first_group, groups, h):
+            chosen = slice(first_group, first_group + groups)
             for r in range(4):
                 nc.sync.dma_start(
-                    out=w_scales[32 * m + r : P : 64, :, :].bitcast(I32),
-                    in_=scale_rows[m, r].bitcast(I32),
+                    out=w_scales[h][r : P : 32, chosen, :].bitcast(I32),
+                    in_=scale_rows[r][:, chosen, h * (F // 2) : (h + 1) * (F // 2)].bitcast(I32),
                 )
-        load_weights(W_SOURCE, 2 * G)
+
+        load_chunk(0)
+        load_scales(W_SOURCE, 2 * G, 0)
+        load_weights(W_SOURCE, 2 * G, 0)
         load_chunk(1)
-        load_weights(W_TARGET, G)
+        load_scales(W_SOURCE, 2 * G, 1)
+        load_weights(W_SOURCE, 2 * G, 1)
+        for h in range(2):
+            load_scales(W_TARGET, G, h)
+            load_weights(W_TARGET, G, h)
+        nc.sync.dma_start(out=bias_rows_bf[0:F_TILES, :], in_=b_pre.rearrange("(t f) -> t f", f=P))
         for c in range(2, CHUNKS):
             load_chunk(c)
 
@@ -120,9 +129,10 @@ def tile_gnnlayer_pa_kernel(tc, x, e_enc, W_pre_words, W_pre_scales, b_pre, out)
             nc.scalar.copy(out=grouped.bitcast(F32), in_=turned[:].rearrange("p g u r -> p g r u"))
 
         def weight(group, ft):
+            h, q = divmod(ft, GROUP_TILES)
             return dict(
-                lhsT=w_words[:, group, 2 * P * ft : 2 * P * (ft + 1)].bitcast(FP4X4),
-                lhsT_scale=w_scales[:, group, P * ft : P * (ft + 1)],
+                lhsT=w_words[h][:, group, 2 * P * q : 2 * P * (q + 1)].bitcast(FP4X4),
+                lhsT_scale=w_scales[h][:, group, P * q : P * (q + 1)],
             )
 
         def repeat_sources(b):
@@ -152,7 +162,26 @@ def tile_gnnlayer_pa_kernel(tc, x, e_enc, W_pre_words, W_pre_scales, b_pre, out)
             )
             return codes, scales
 
+        def first_chunk():
+            codes = work.tile([P, G, CHUNK], U32, align_bytes=64)
+            scales = work.tile([P, G, CHUNK], U8, align_bytes=64)
+            for t in range(ROW_TILES):
+                part = keep.tile([P, G, P, PACK], BF16, align_bytes=64, name="first_rows_%d" % t)
+                k_onto_partitions(e_raw[:, 0, t, :], part[:])
+                rows = slice(t * P, (t + 1) * P)
+                for g in range(G):
+                    nc.vector.quantize_mx(
+                        out=codes[:, g, rows].bitcast(FP8X4),
+                        scales=scales[:, g, rows],
+                        in_=part[:, g, :, :].rearrange("p e t -> p (e t)"),
+                    )
+            return codes, scales
+
         def target_terms():
+            nc.scalar.copy(out=bias_rows[:], in_=bias_rows_bf[:])
+            bias_turned = psum_aux.tile([P, GROUP_TILES, P], F32, tag="bank")
+            nc.tensor.transpose(bias_turned[:, 0, :], bias_rows[:], ident[:])
+            nc.scalar.copy(out=bias_col[:], in_=bias_turned[:, 0, 0:F_TILES])
             for h in range(GROUPS_PER_CHUNK):
                 target_term = psum_aux.tile([P, GROUP_TILES, P], F32, tag="bank")
                 for q in range(GROUP_TILES):
@@ -218,26 +247,29 @@ def tile_gnnlayer_pa_kernel(tc, x, e_enc, W_pre_words, W_pre_scales, b_pre, out)
             return clipped
 
         def larger_and_smaller(copies, clipped):
-            sorted_pairs = stage.tile([P, SHARED_ROWS, 2, HALF], F32)
+            sorted_pairs = stage.tile([P, 2, SHARED_ROWS, HALF], F32)
             nc.gpsimd.tensor_tensor(
-                out=sorted_pairs[:, :, 0, :], in0=copies[:, :, 0:HALF], in1=clipped[:], op=ALU.add
+                out=sorted_pairs[:, 0, :, :], in0=copies[:, :, 0:HALF], in1=clipped[:], op=ALU.add
             )
             nc.gpsimd.tensor_tensor(
-                out=sorted_pairs[:, :, 1, :], in0=copies[:, :, HALF:N], in1=clipped[:], op=ALU.subtract
+                out=sorted_pairs[:, 1, :, :], in0=copies[:, :, HALF:N], in1=clipped[:], op=ALU.subtract
             )
             return sorted_pairs
 
-        def shared_extremes(sorted_pairs, h, stats, first_target):
+        def shared_extreme(sorted_pairs, smaller, h, stats, first_target):
             results = stats[1]
             first = h * GROUP_TILES + SHARED_TILES[0]
             last = h * GROUP_TILES + SHARED_TILES[-1]
             tiles = slice(first, last + 1, SHARED_TILES[1] - SHARED_TILES[0])
             targets = slice(first_target, first_target + TARGETS)
-            pairs = sorted_pairs[:].rearrange("p (n i) m k -> p n i m k", i=TARGETS)
-            nc.vector.tensor_reduce(out=results[:, tiles, 2, targets], in_=pairs[:, :, :, 0, :], axis=AXIS.X, op=ALU.max)
-            nc.vector.tensor_reduce(out=results[:, tiles, 1, targets], in_=pairs[:, :, :, 1, :], axis=AXIS.X, op=ALU.min)
+            nc.vector.tensor_reduce(
+                out=results[:, tiles, 2 - smaller, targets],
+                in_=sorted_pairs[:, smaller, :, :].rearrange("p (n i) k -> p n i k", i=TARGETS),
+                axis=AXIS.X,
+                op=(ALU.max, ALU.min)[smaller],
+            )
 
-        def aggregate(banks, copies, h, stats, first_target, moments=True, extremes=True, turned_chunk=None):
+        def aggregate(banks, copies, h, stats, first_target, moments=True, extremes=True, turned_chunk=None, inserts=None):
             s_moments, results = stats
             targets = slice(first_target, first_target + TARGETS)
             quantised = None
@@ -259,6 +291,8 @@ def tile_gnnlayer_pa_kernel(tc, x, e_enc, W_pre_words, W_pre_scales, b_pre, out)
                     nc.vector.tensor_reduce(out=results[:, ft, 1, targets], in_=s, axis=AXIS.X, op=ALU.min)
                 if q == 1 and turned_chunk is not None:
                     quantised = quantise_chunk(turned_chunk)
+                for older in (inserts or {}).get(q, []):
+                    shared_extreme(*older)
             return quantised
 
         def finish_moments(b, h, stats):
@@ -298,20 +332,18 @@ def tile_gnnlayer_pa_kernel(tc, x, e_enc, W_pre_words, W_pre_scales, b_pre, out)
                 nc.sync.dma_start(out=out[b, :, first : first + CHUNK], in_=rows[a * N : (a + 1) * N, :])
 
         k_onto_partitions(x_raw[:], x_grouped[:])
-        nc.vector.tensor_copy(out=bias_rows[:], in_=bias_rows_bf[:])
-        bias_turned = psum_aux.tile([P, GROUP_TILES, P], F32, tag="bank")
-        nc.tensor.transpose(bias_turned[:, 0, :], bias_rows[:], ident[:])
         nc.vector.quantize_mx(
             out=x_codes[:].rearrange("p g r -> p (g r)").bitcast(FP8X4),
             scales=x_scales[:].rearrange("p g r -> p (g r)"),
             in_=x_grouped[:].rearrange("p g r t -> p (g r t)"),
         )
-        nc.vector.tensor_copy(out=bias_col[:], in_=bias_turned[:, 0, 0:F_TILES])
 
-        for b in range(B):
+        for b in range(B // 2):
             repeat_sources(b)
 
-        following = quantise_chunk(turn_chunk(0))
+        following = first_chunk()
+        for b in range(B // 2, B):
+            repeat_sources(b)
         turned_chunk = None
         current = None
         graph_stats = {}
@@ -326,7 +358,7 @@ def tile_gnnlayer_pa_kernel(tc, x, e_enc, W_pre_words, W_pre_scales, b_pre, out)
                 results = work.tile([P, F_TILES, AGGREGATORS, N], F32)
                 graph_stats[b] = (s_moments, results)
             stats = graph_stats[b]
-            shared = step < GROUPS - SHARE_LAG
+            shared = step < GROUPS - 1
             if step - 1 in in_flight:
                 in_flight[step - 1].append(clip(in_flight[step - 1][1]))
             banks, copies = messages(b, h, current[0], current[1], shared)
@@ -336,26 +368,39 @@ def tile_gnnlayer_pa_kernel(tc, x, e_enc, W_pre_words, W_pre_scales, b_pre, out)
             if shared:
                 in_flight[step] = [copies, differences(copies)]
             if step < GROUPS - 1:
-                quantised = aggregate(banks, copies, h, stats, part * TARGETS, turned_chunk=turned_chunk)
+                inserts = {}
+                if step - SHARE_LAG in in_flight:
+                    older_c, older_h = divmod(step - SHARE_LAG, GROUPS_PER_CHUNK)
+                    older_b, older_part = divmod(older_c, CHUNKS_PER_GRAPH)
+                    older = (older_h, graph_stats[older_b], older_part * TARGETS)
+                    inserts[2] = [(in_flight[step - SHARE_LAG][3], 0) + older]
+                    inserts[3] = [(in_flight[step - SHARE_LAG][3], 1) + older]
+                quantised = aggregate(
+                    banks, copies, h, stats, part * TARGETS, turned_chunk=turned_chunk, inserts=inserts
+                )
                 if quantised is not None:
                     following = quantised
                     turned_chunk = None
             else:
+                last = in_flight[step - 1]
+                last.append(larger_and_smaller(last[0], last[2]))
                 finish_moments(b, h - 1, stats)
-                finish_store(b, h - 1, stats)
                 aggregate(banks, copies, h, stats, part * TARGETS, extremes=False)
                 finish_moments(b, h, stats)
-                aggregate(banks, copies, h, stats, part * TARGETS, moments=False)
-                shared_extremes(in_flight[step - SHARE_LAG][3], h, stats, 0)
+                before_last = in_flight[step - SHARE_LAG][3]
+                inserts = {
+                    0: [(before_last, 0, h, stats, 0)],
+                    1: [(before_last, 1, h, stats, 0)],
+                    2: [(last[3], 0, h - 1, stats, part * TARGETS)],
+                }
+                aggregate(banks, copies, h, stats, part * TARGETS, moments=False, inserts=inserts)
                 finish_store(b, h, stats)
+                shared_extreme(last[3], 1, h - 1, stats, part * TARGETS)
+                finish_store(b, h - 1, stats)
             if h == 0 and c + 1 < CHUNKS:
                 turned_chunk = turn_chunk(c + 1)
             if step == TARGET_TERMS_STEP:
                 target_terms()
-            if step - SHARE_LAG in in_flight and step < GROUPS - 1:
-                c, h = divmod(step - SHARE_LAG, GROUPS_PER_CHUNK)
-                b, part = divmod(c, CHUNKS_PER_GRAPH)
-                shared_extremes(in_flight[step - SHARE_LAG][3], h, graph_stats[b], part * TARGETS)
             for done in range(GROUPS - GROUPS_PER_CHUNK):
                 c, h = divmod(done, GROUPS_PER_CHUNK)
                 b, part = divmod(c, CHUNKS_PER_GRAPH)

@@ -51,6 +51,7 @@ def tile_gnnlayer_pa_kernel(tc, x, e_enc, W_pre_words, W_pre_scales, b_pre, out)
         work = ctx.enter_context(tc.tile_pool(name="work", bufs=2))
         stream = ctx.enter_context(tc.tile_pool(name="stream", bufs=3))
         stage = ctx.enter_context(tc.tile_pool(name="stage", bufs=2))
+        handover = ctx.enter_context(tc.tile_pool(name="handover", bufs=1))
         psum_msg = ctx.enter_context(tc.psum_pool(name="psum_msg", bufs=4))
         psum_aux = ctx.enter_context(tc.psum_pool(name="psum_aux", bufs=4))
 
@@ -147,7 +148,7 @@ def tile_gnnlayer_pa_kernel(tc, x, e_enc, W_pre_words, W_pre_scales, b_pre, out)
             )
 
         def turn_chunk(c):
-            grouped = work.tile([P, G, CHUNK, PACK], BF16, align_bytes=64)
+            grouped = handover.tile([P, G, CHUNK, PACK], BF16, align_bytes=64, tag="turn")
             for t in range(ROW_TILES):
                 k_onto_partitions(e_raw[:, c, t, :], grouped[:, :, t * P : (t + 1) * P, :])
             return grouped
@@ -234,8 +235,11 @@ def tile_gnnlayer_pa_kernel(tc, x, e_enc, W_pre_words, W_pre_scales, b_pre, out)
                 banks.append(bank)
             return banks, copies
 
-        def differences(copies):
-            apart = stage.tile([P, SHARED_ROWS, HALF], F32)
+        def differences(copies, behind_quantize=False):
+            if behind_quantize:
+                apart = handover.tile([P, SHARED_ROWS, HALF], F32, align_bytes=64, tag="turn")
+            else:
+                apart = stage.tile([P, SHARED_ROWS, HALF], F32)
             nc.gpsimd.tensor_tensor(
                 out=apart[:], in0=copies[:, :, HALF:N], in1=copies[:, :, 0:HALF], op=ALU.subtract
             )
@@ -273,6 +277,7 @@ def tile_gnnlayer_pa_kernel(tc, x, e_enc, W_pre_words, W_pre_scales, b_pre, out)
             s_moments, results = stats
             targets = slice(first_target, first_target + TARGETS)
             quantised = None
+            apart = None
             for q in range(GROUP_TILES):
                 ft = h * GROUP_TILES + q
                 s = banks[q][:].rearrange("p (i j) -> p i j", j=N)
@@ -289,11 +294,13 @@ def tile_gnnlayer_pa_kernel(tc, x, e_enc, W_pre_words, W_pre_scales, b_pre, out)
                 if extremes and not shared:
                     nc.vector.tensor_reduce(out=results[:, ft, 2, targets], in_=s, axis=AXIS.X, op=ALU.max)
                     nc.vector.tensor_reduce(out=results[:, ft, 1, targets], in_=s, axis=AXIS.X, op=ALU.min)
-                if q == 1 and turned_chunk is not None:
+                if q == 0 and turned_chunk is not None:
                     quantised = quantise_chunk(turned_chunk)
+                    if copies is not None:
+                        apart = differences(copies, behind_quantize=True)
                 for older in (inserts or {}).get(q, []):
                     shared_extreme(*older)
-            return quantised
+            return quantised, apart
 
         def finish_moments(b, h, stats):
             s_moments, results = stats
@@ -365,7 +372,7 @@ def tile_gnnlayer_pa_kernel(tc, x, e_enc, W_pre_words, W_pre_scales, b_pre, out)
             if step - SHARE_LAG in in_flight:
                 earlier = in_flight[step - SHARE_LAG]
                 earlier.append(larger_and_smaller(earlier[0], earlier[2]))
-            if shared:
+            if shared and turned_chunk is None:
                 in_flight[step] = [copies, differences(copies)]
             if step < GROUPS - 1:
                 inserts = {}
@@ -375,12 +382,13 @@ def tile_gnnlayer_pa_kernel(tc, x, e_enc, W_pre_words, W_pre_scales, b_pre, out)
                     older = (older_h, graph_stats[older_b], older_part * TARGETS)
                     inserts[2] = [(in_flight[step - SHARE_LAG][3], 0) + older]
                     inserts[3] = [(in_flight[step - SHARE_LAG][3], 1) + older]
-                quantised = aggregate(
+                quantised, apart = aggregate(
                     banks, copies, h, stats, part * TARGETS, turned_chunk=turned_chunk, inserts=inserts
                 )
                 if quantised is not None:
                     following = quantised
                     turned_chunk = None
+                    in_flight[step] = [copies, apart]
             else:
                 last = in_flight[step - 1]
                 last.append(larger_and_smaller(last[0], last[2]))

@@ -70,8 +70,10 @@ def tile_gnnlayer_pa_kernel(tc, x, e_enc, W_pre_words, W_pre_scales, b_pre, out)
         bias_col = keep.tile([P, F_TILES], F32)
         base = keep.tile([P, F_TILES, B, AGGREGATORS, N], F32)
         eps = keep.tile([P, 1], F32)
+        idle_operand = keep.tile([P, CHUNK], BF16)
         warm = keep.tile([P, 1], F32)
 
+        nc.gpsimd.memset(idle_operand[:], 0.0)
         for h in range(2):
             nc.vector.memset(w_scales[h][:].bitcast(I32), 0)
         nc.vector.memset(x_scales[:].bitcast(I32), 0)
@@ -129,6 +131,11 @@ def tile_gnnlayer_pa_kernel(tc, x, e_enc, W_pre_words, W_pre_scales, b_pre, out)
                     )
             nc.scalar.copy(out=grouped.bitcast(F32), in_=turned[:].rearrange("p g u r -> p g r u"))
 
+        def keep_clock_up(matmuls):
+            bank = psum_msg.tile([P, CHUNK], F32)
+            for n in range(matmuls):
+                nc.tensor.matmul(bank[:], lhsT=idle_operand[:, 0:P], rhs=idle_operand[:], start=True, stop=True)
+
         def weight(group, ft):
             h, q = divmod(ft, GROUP_TILES)
             return dict(
@@ -169,6 +176,7 @@ def tile_gnnlayer_pa_kernel(tc, x, e_enc, W_pre_words, W_pre_scales, b_pre, out)
             for t in range(ROW_TILES):
                 part = keep.tile([P, G, P, PACK], BF16, align_bytes=64, name="first_rows_%d" % t)
                 k_onto_partitions(e_raw[:, 0, t, :], part[:])
+                keep_clock_up(1 if t < ROW_TILES - 1 else 2)
                 rows = slice(t * P, (t + 1) * P)
                 for g in range(G):
                     nc.vector.quantize_mx(
@@ -338,7 +346,9 @@ def tile_gnnlayer_pa_kernel(tc, x, e_enc, W_pre_words, W_pre_scales, b_pre, out)
                 first = a * F + h * CHUNK
                 nc.sync.dma_start(out=out[b, :, first : first + CHUNK], in_=rows[a * N : (a + 1) * N, :])
 
+        keep_clock_up(3)
         k_onto_partitions(x_raw[:], x_grouped[:])
+        keep_clock_up(1)
         nc.vector.quantize_mx(
             out=x_codes[:].rearrange("p g r -> p (g r)").bitcast(FP8X4),
             scales=x_scales[:].rearrange("p g r -> p (g r)"),

@@ -34,17 +34,18 @@ GROUPS_PER_CHUNK = F_TILES // GROUP_TILES
 GROUPS = CHUNKS * GROUPS_PER_CHUNK
 MOMENTS = 3
 FINISH_LAG = 2
-SHARED_TILES = (1, 2, 3)
+SHARED_TILES = ((2, 3), (1, 2, 3))
 SHARE_LAG = 2
 HALF = N // 2
-TARGET_TERMS_STEP = 1
+TARGET_TERMS_STEP = 3
+SUMMED_TILE = 0
+RAW_CHUNKS = 4
 
 FLOPS = 2 * (B * N * N + 2 * B * N) * C * F
 
 
 def tile_gnnlayer_pa_kernel(tc, x, e_enc, W_pre_words, W_pre_scales, b_pre, out):
     nc = tc.nc
-    SHARED_ROWS = len(SHARED_TILES) * TARGETS
     with ExitStack() as ctx:
         ctx.enter_context(tc.manual_schedule())
         keep = ctx.enter_context(tc.tile_pool(name="keep", bufs=1))
@@ -52,11 +53,15 @@ def tile_gnnlayer_pa_kernel(tc, x, e_enc, W_pre_words, W_pre_scales, b_pre, out)
         stream = ctx.enter_context(tc.tile_pool(name="stream", bufs=3))
         stage = ctx.enter_context(tc.tile_pool(name="stage", bufs=2))
         handover = ctx.enter_context(tc.tile_pool(name="handover", bufs=1))
+        raw = ctx.enter_context(tc.tile_pool(name="raw", bufs=RAW_CHUNKS))
         psum_msg = ctx.enter_context(tc.psum_pool(name="psum_msg", bufs=4))
         psum_aux = ctx.enter_context(tc.psum_pool(name="psum_aux", bufs=4))
 
         x_raw = keep.tile([P, C], BF16)
-        e_raw = keep.tile([P, CHUNKS, ROW_TILES, C], BF16)
+        e_raw = {}
+        by_source = keep.tile([P, 2, N, P], F32)
+        plain_base = keep.tile([P, P], F32)
+        zeros = keep.tile([P, 2, N], F32)
         w_words = [keep.tile([P, 3 * G, F], U8, align_bytes=64, name="w_words_%d" % h) for h in range(2)]
         w_scales = [keep.tile([P, 3 * G, F // 2], U8, align_bytes=64, name="w_scales_%d" % h) for h in range(2)]
         x_grouped = keep.tile([P, G, P, PACK], BF16, align_bytes=64)
@@ -81,15 +86,18 @@ def tile_gnnlayer_pa_kernel(tc, x, e_enc, W_pre_words, W_pre_scales, b_pre, out)
         nc.vector.memset(eps[:], EPS_STD)
         make_identity(nc, ident[:])
         nc.gpsimd.memset(base[:, :, :, 3, :], 0.0)
+        nc.gpsimd.memset(zeros[:], 0.0)
         nc.scalar.activation(out=warm[:], in_=eps[:], func=ACT.Sqrt)
 
         nc.sync.dma_start(out=x_raw[:], in_=x.rearrange("b n c -> (b n) c"))
         edges = e_enc.rearrange("b i j c -> (b i j) c")
 
         def load_chunk(c):
+            rows = raw.tile([P, ROW_TILES, C], BF16)
             for t in range(ROW_TILES):
                 first_row = c * CHUNK + t * P
-                nc.sync.dma_start(out=e_raw[:, c, t, :], in_=edges[first_row : first_row + P, :])
+                nc.sync.dma_start(out=rows[:, t, :], in_=edges[first_row : first_row + P, :])
+            e_raw[c] = rows
 
         def load_weights(first_group, groups, h):
             chosen = slice(first_group, first_group + groups)
@@ -118,7 +126,7 @@ def tile_gnnlayer_pa_kernel(tc, x, e_enc, W_pre_words, W_pre_scales, b_pre, out)
             load_scales(W_TARGET, G, h)
             load_weights(W_TARGET, G, h)
         nc.sync.dma_start(out=bias_rows_bf[0:F_TILES, :], in_=b_pre.rearrange("(t f) -> t f", f=P))
-        for c in range(2, CHUNKS):
+        for c in range(2, RAW_CHUNKS):
             load_chunk(c)
 
         def k_onto_partitions(rows_bf16, grouped):
@@ -157,7 +165,9 @@ def tile_gnnlayer_pa_kernel(tc, x, e_enc, W_pre_words, W_pre_scales, b_pre, out)
         def turn_chunk(c):
             grouped = handover.tile([P, G, CHUNK, PACK], BF16, align_bytes=64, tag="turn")
             for t in range(ROW_TILES):
-                k_onto_partitions(e_raw[:, c, t, :], grouped[:, :, t * P : (t + 1) * P, :])
+                k_onto_partitions(e_raw[c][:, t, :], grouped[:, :, t * P : (t + 1) * P, :])
+            if c + RAW_CHUNKS < CHUNKS:
+                load_chunk(c + RAW_CHUNKS)
             return grouped
 
         def quantise_chunk(grouped):
@@ -175,7 +185,7 @@ def tile_gnnlayer_pa_kernel(tc, x, e_enc, W_pre_words, W_pre_scales, b_pre, out)
             scales = work.tile([P, G, CHUNK], U8, align_bytes=64)
             for t in range(ROW_TILES):
                 part = keep.tile([P, G, P, PACK], BF16, align_bytes=64, name="first_rows_%d" % t)
-                k_onto_partitions(e_raw[:, 0, t, :], part[:])
+                k_onto_partitions(e_raw[0][:, t, :], part[:])
                 keep_clock_up(1 if t < ROW_TILES - 1 else 2)
                 rows = slice(t * P, (t + 1) * P)
                 for g in range(G):
@@ -184,6 +194,7 @@ def tile_gnnlayer_pa_kernel(tc, x, e_enc, W_pre_words, W_pre_scales, b_pre, out)
                         scales=scales[:, g, rows],
                         in_=part[:, g, :, :].rearrange("p e t -> p (e t)"),
                     )
+            load_chunk(RAW_CHUNKS)
             return codes, scales
 
         def target_terms():
@@ -215,14 +226,23 @@ def tile_gnnlayer_pa_kernel(tc, x, e_enc, W_pre_words, W_pre_scales, b_pre, out)
                         bias=bias_col[:, ft : ft + 1],
                         scale=1.0,
                     )
+                    if ft == SUMMED_TILE:
+                        nc.scalar.activation(
+                            out=plain_base[:],
+                            in_=target_term[:, q, :],
+                            func=ACT.Identity,
+                            bias=bias_col[:, ft : ft + 1],
+                            scale=1.0,
+                        )
 
-        def messages(b, h, codes, scales, shared):
+        def messages(c, h, codes, scales, tiles):
+            b = c // CHUNKS_PER_GRAPH
             moving = [(W_SOURCE + g, src_codes[:, b, g, :], src_scales[:, b, g, :]) for g in range(G)]
             moving += [(W_EDGE + g, codes[:, g, :], scales[:, g, :]) for g in range(G)]
             banks = []
             copies = None
-            if shared:
-                copies = stream.tile([P, SHARED_ROWS, N], F32)
+            if tiles:
+                copies = stream.tile([P, len(tiles) * TARGETS, N], F32)
             for q in range(GROUP_TILES):
                 bank = psum_msg.tile([P, CHUNK], F32)
                 for n, (group, rhs, rhs_scale) in enumerate(moving):
@@ -234,8 +254,8 @@ def tile_gnnlayer_pa_kernel(tc, x, e_enc, W_pre_words, W_pre_scales, b_pre, out)
                         stop=(n == len(moving) - 1),
                         **weight(group, h * GROUP_TILES + q),
                     )
-                if shared and q in SHARED_TILES:
-                    slot = SHARED_TILES.index(q)
+                if q in tiles:
+                    slot = tiles.index(q)
                     nc.scalar.copy(
                         out=copies[:, slot * TARGETS : (slot + 1) * TARGETS, :].rearrange("p i j -> p (i j)"),
                         in_=bank[:],
@@ -243,23 +263,23 @@ def tile_gnnlayer_pa_kernel(tc, x, e_enc, W_pre_words, W_pre_scales, b_pre, out)
                 banks.append(bank)
             return banks, copies
 
-        def differences(copies, behind_quantize=False):
+        def differences(copies, rows, behind_quantize=False):
             if behind_quantize:
-                apart = handover.tile([P, SHARED_ROWS, HALF], F32, align_bytes=64, tag="turn")
+                apart = handover.tile([P, rows, HALF], F32, align_bytes=64, tag="turn")
             else:
-                apart = stage.tile([P, SHARED_ROWS, HALF], F32)
+                apart = stage.tile([P, rows, HALF], F32)
             nc.gpsimd.tensor_tensor(
                 out=apart[:], in0=copies[:, :, HALF:N], in1=copies[:, :, 0:HALF], op=ALU.subtract
             )
             return apart
 
-        def clip(apart):
-            clipped = stage.tile([P, SHARED_ROWS, HALF], F32)
+        def clip(apart, rows):
+            clipped = stage.tile([P, rows, HALF], F32)
             nc.scalar.activation(out=clipped[:], in_=apart[:], func=ACT.Relu)
             return clipped
 
-        def larger_and_smaller(copies, clipped):
-            sorted_pairs = stage.tile([P, 2, SHARED_ROWS, HALF], F32)
+        def larger_and_smaller(copies, clipped, rows):
+            sorted_pairs = stage.tile([P, 2, rows, HALF], F32)
             nc.gpsimd.tensor_tensor(
                 out=sorted_pairs[:, 0, :, :], in0=copies[:, :, 0:HALF], in1=clipped[:], op=ALU.add
             )
@@ -270,9 +290,7 @@ def tile_gnnlayer_pa_kernel(tc, x, e_enc, W_pre_words, W_pre_scales, b_pre, out)
 
         def shared_extreme(sorted_pairs, smaller, h, stats, first_target):
             results = stats[1]
-            first = h * GROUP_TILES + SHARED_TILES[0]
-            last = h * GROUP_TILES + SHARED_TILES[-1]
-            tiles = slice(first, last + 1, SHARED_TILES[1] - SHARED_TILES[0])
+            tiles = slice(h * GROUP_TILES + SHARED_TILES[h][0], h * GROUP_TILES + SHARED_TILES[h][-1] + 1)
             targets = slice(first_target, first_target + TARGETS)
             nc.vector.tensor_reduce(
                 out=results[:, tiles, 2 - smaller, targets],
@@ -281,7 +299,9 @@ def tile_gnnlayer_pa_kernel(tc, x, e_enc, W_pre_words, W_pre_scales, b_pre, out)
                 op=(ALU.max, ALU.min)[smaller],
             )
 
-        def aggregate(banks, copies, h, stats, first_target, moments=True, extremes=True, turned_chunk=None, inserts=None):
+        def aggregate(
+            banks, copies, h, stats, first_target, moments=True, extremes=True, turned_chunk=None, inserts=None, graph=0
+        ):
             s_moments, results = stats
             targets = slice(first_target, first_target + TARGETS)
             quantised = None
@@ -289,34 +309,45 @@ def tile_gnnlayer_pa_kernel(tc, x, e_enc, W_pre_words, W_pre_scales, b_pre, out)
             for q in range(GROUP_TILES):
                 ft = h * GROUP_TILES + q
                 s = banks[q][:].rearrange("p (i j) -> p i j", j=N)
-                shared = copies is not None and q in SHARED_TILES
+                shared = copies is not None and q in SHARED_TILES[h]
                 if shared:
-                    slot = SHARED_TILES.index(q)
+                    slot = SHARED_TILES[h].index(q)
                     s = copies[:, slot * TARGETS : (slot + 1) * TARGETS, :]
-                for pair in range(TARGETS // 2 if moments else 0):
+                summed = ft == SUMMED_TILE
+                for pair in range(TARGETS // 2 if moments and not summed else 0):
                     first = MOMENTS * (first_target + 2 * pair)
                     nc.vector.bn_stats(
                         out=s_moments[:, ft, first : first + 2 * MOMENTS],
                         in_=s[:, 2 * pair : 2 * pair + 2, :].rearrange("p i j -> p j i"),
                     )
-                if extremes and not shared:
+                if (moments if summed else extremes) and not shared:
                     nc.vector.tensor_reduce(out=results[:, ft, 2, targets], in_=s, axis=AXIS.X, op=ALU.max)
                     nc.vector.tensor_reduce(out=results[:, ft, 1, targets], in_=s, axis=AXIS.X, op=ALU.min)
+                if summed and moments:
+                    columns = slice(graph * N + first_target, graph * N + first_target + TARGETS)
+                    source_first = banks[q][:].rearrange("p (i j) -> p j i", j=N)
+                    nc.scalar.copy(out=by_source[:, 0, :, columns], in_=source_first)
+                    nc.scalar.activation(out=by_source[:, 1, :, columns], in_=source_first, func=ACT.Square)
                 if q == 0 and turned_chunk is not None:
                     quantised = quantise_chunk(turned_chunk)
                     if copies is not None:
-                        apart = differences(copies, behind_quantize=True)
+                        apart = differences(copies, len(SHARED_TILES[h]) * TARGETS, behind_quantize=True)
                 for older in (inserts or {}).get(q, []):
                     shared_extreme(*older)
             return quantised, apart
 
         def finish_moments(b, h, stats):
             s_moments, results = stats
-            tiles = slice(h * GROUP_TILES, (h + 1) * GROUP_TILES)
+            first = h * GROUP_TILES
+            if first == SUMMED_TILE:
+                nc.scalar.copy(out=results[:, first, 0:AGGREGATORS:3, :], in_=zeros[:])
+                first += 1
+            tiles = slice(first, (h + 1) * GROUP_TILES)
             moments = s_moments[:, tiles, :].rearrange("p q (i m) -> p q i m", m=MOMENTS)
             variance = work.tile([P, GROUP_TILES, N], F32)
-            nc.scalar.activation(out=variance[:], in_=moments[:, :, :, 2], func=ACT.Relu, scale=1.0 / N)
-            nc.scalar.activation(out=results[:, tiles, 3, :], in_=variance[:], func=ACT.Sqrt, bias=eps[:])
+            count = (h + 1) * GROUP_TILES - first
+            nc.scalar.activation(out=variance[:, 0:count, :], in_=moments[:, :, :, 2], func=ACT.Relu, scale=1.0 / N)
+            nc.scalar.activation(out=results[:, tiles, 3, :], in_=variance[:, 0:count, :], func=ACT.Sqrt, bias=eps[:])
             nc.scalar.copy(out=results[:, tiles, 0, :], in_=moments[:, :, :, 1])
 
         def finish_store(b, h, stats):
@@ -344,7 +375,40 @@ def tile_gnnlayer_pa_kernel(tc, x, e_enc, W_pre_words, W_pre_scales, b_pre, out)
             nc.scalar.copy(out=rows[:], in_=turned[:].rearrange("p q f -> p (q f)"))
             for a in range(AGGREGATORS):
                 first = a * F + h * CHUNK
-                nc.sync.dma_start(out=out[b, :, first : first + CHUNK], in_=rows[a * N : (a + 1) * N, :])
+                skip = P if h * GROUP_TILES == SUMMED_TILE and a in (0, 3) else 0
+                nc.sync.dma_start(
+                    out=out[b, :, first + skip : first + CHUNK], in_=rows[a * N : (a + 1) * N, skip:CHUNK]
+                )
+
+        def summed_moments():
+            sums = psum_aux.tile([P, GROUP_TILES, P], F32, tag="bank")
+            for k in range(2):
+                for j in range(N):
+                    nc.tensor.matmul(
+                        sums[:, k, :],
+                        lhsT=by_source[:, k, j, :],
+                        rhs=ident[:],
+                        is_transpose=True,
+                        start=(j == 0),
+                        stop=(j == N - 1),
+                    )
+            nc.tensor.transpose(sums[:, 2, :], plain_base[:], ident[:])
+            pieces = keep.tile([P, 8, P], F32)
+            mean_s, mean_squared, second, base_turned, variance, mean, clipped, deviation = [
+                pieces[:, n, :] for n in range(8)
+            ]
+            nc.scalar.activation(out=mean_s, in_=sums[:, 0, :], func=ACT.Copy, scale=1.0 / N)
+            nc.scalar.activation(out=mean_squared, in_=sums[:, 0, :], func=ACT.Square, scale=1.0 / N)
+            nc.scalar.activation(out=second, in_=sums[:, 1, :], func=ACT.Copy, scale=1.0 / N)
+            nc.scalar.copy(out=base_turned, in_=sums[:, 2, :])
+            nc.gpsimd.tensor_tensor(out=variance, in0=second, in1=mean_squared, op=ALU.subtract)
+            nc.gpsimd.tensor_tensor(out=mean, in0=mean_s, in1=base_turned, op=ALU.add)
+            nc.scalar.activation(out=clipped, in_=variance, func=ACT.Relu)
+            nc.scalar.activation(out=deviation, in_=clipped, func=ACT.Sqrt, bias=eps[:])
+            all_targets = out.rearrange("b i f -> (b i) f")
+            nc.sync.dma_start(out=all_targets[:, SUMMED_TILE * P : (SUMMED_TILE + 1) * P], in_=mean)
+            first = 3 * F + SUMMED_TILE * P
+            nc.sync.dma_start(out=all_targets[:, first : first + P], in_=deviation)
 
         keep_clock_up(3)
         k_onto_partitions(x_raw[:], x_grouped[:])
@@ -376,14 +440,16 @@ def tile_gnnlayer_pa_kernel(tc, x, e_enc, W_pre_words, W_pre_scales, b_pre, out)
                 graph_stats[b] = (s_moments, results)
             stats = graph_stats[b]
             shared = step < GROUPS - 1
+            rows = len(SHARED_TILES[h]) * TARGETS
+            other_rows = len(SHARED_TILES[1 - h]) * TARGETS
             if step - 1 in in_flight:
-                in_flight[step - 1].append(clip(in_flight[step - 1][1]))
-            banks, copies = messages(b, h, current[0], current[1], shared)
+                in_flight[step - 1].append(clip(in_flight[step - 1][1], other_rows))
+            banks, copies = messages(c, h, current[0], current[1], SHARED_TILES[h] if shared else ())
             if step - SHARE_LAG in in_flight:
                 earlier = in_flight[step - SHARE_LAG]
-                earlier.append(larger_and_smaller(earlier[0], earlier[2]))
+                earlier.append(larger_and_smaller(earlier[0], earlier[2], rows))
             if shared and turned_chunk is None:
-                in_flight[step] = [copies, differences(copies)]
+                in_flight[step] = [copies, differences(copies, rows)]
             if step < GROUPS - 1:
                 inserts = {}
                 if step - SHARE_LAG in in_flight:
@@ -393,7 +459,7 @@ def tile_gnnlayer_pa_kernel(tc, x, e_enc, W_pre_words, W_pre_scales, b_pre, out)
                     inserts[2] = [(in_flight[step - SHARE_LAG][3], 0) + older]
                     inserts[3] = [(in_flight[step - SHARE_LAG][3], 1) + older]
                 quantised, apart = aggregate(
-                    banks, copies, h, stats, part * TARGETS, turned_chunk=turned_chunk, inserts=inserts
+                    banks, copies, h, stats, part * TARGETS, turned_chunk=turned_chunk, inserts=inserts, graph=b
                 )
                 if quantised is not None:
                     following = quantised
@@ -401,10 +467,11 @@ def tile_gnnlayer_pa_kernel(tc, x, e_enc, W_pre_words, W_pre_scales, b_pre, out)
                     in_flight[step] = [copies, apart]
             else:
                 last = in_flight[step - 1]
-                last.append(larger_and_smaller(last[0], last[2]))
+                last.append(larger_and_smaller(last[0], last[2], other_rows))
                 finish_moments(b, h - 1, stats)
-                aggregate(banks, copies, h, stats, part * TARGETS, extremes=False)
+                aggregate(banks, copies, h, stats, part * TARGETS, extremes=False, graph=b)
                 finish_moments(b, h, stats)
+                summed_moments()
                 before_last = in_flight[step - SHARE_LAG][3]
                 inserts = {
                     0: [(before_last, 0, h, stats, 0)],

@@ -34,7 +34,8 @@ GROUPS_PER_CHUNK = F_TILES // GROUP_TILES
 GROUPS = CHUNKS * GROUPS_PER_CHUNK
 MOMENTS = 3
 FINISH_LAG = 2
-SHARED_TILES = ((2, 3), (1, 2, 3))
+SHARED_TILES = (1, 2, 3)
+FEWER_SHARED_TILES = (2, 3)
 SHARE_LAG = 2
 HALF = N // 2
 TARGET_TERMS_STEP = 3
@@ -288,9 +289,9 @@ def tile_gnnlayer_pa_kernel(tc, x, e_enc, W_pre_words, W_pre_scales, b_pre, out)
             )
             return sorted_pairs
 
-        def shared_extreme(sorted_pairs, smaller, h, stats, first_target):
+        def shared_extreme(sorted_pairs, smaller, h, stats, first_target, shared_tiles):
             results = stats[1]
-            tiles = slice(h * GROUP_TILES + SHARED_TILES[h][0], h * GROUP_TILES + SHARED_TILES[h][-1] + 1)
+            tiles = slice(h * GROUP_TILES + shared_tiles[0], h * GROUP_TILES + shared_tiles[-1] + 1)
             targets = slice(first_target, first_target + TARGETS)
             nc.vector.tensor_reduce(
                 out=results[:, tiles, 2 - smaller, targets],
@@ -300,7 +301,8 @@ def tile_gnnlayer_pa_kernel(tc, x, e_enc, W_pre_words, W_pre_scales, b_pre, out)
             )
 
         def aggregate(
-            banks, copies, h, stats, first_target, moments=True, extremes=True, turned_chunk=None, inserts=None, graph=0
+            banks, copies, h, stats, first_target, moments=True, extremes=True, turned_chunk=None, inserts=None, graph=0,
+            tiles=(),
         ):
             s_moments, results = stats
             targets = slice(first_target, first_target + TARGETS)
@@ -309,9 +311,9 @@ def tile_gnnlayer_pa_kernel(tc, x, e_enc, W_pre_words, W_pre_scales, b_pre, out)
             for q in range(GROUP_TILES):
                 ft = h * GROUP_TILES + q
                 s = banks[q][:].rearrange("p (i j) -> p i j", j=N)
-                shared = copies is not None and q in SHARED_TILES[h]
+                shared = q in tiles
                 if shared:
-                    slot = SHARED_TILES[h].index(q)
+                    slot = tiles.index(q)
                     s = copies[:, slot * TARGETS : (slot + 1) * TARGETS, :]
                 summed = ft == SUMMED_TILE
                 for pair in range(TARGETS // 2 if moments and not summed else 0):
@@ -331,7 +333,7 @@ def tile_gnnlayer_pa_kernel(tc, x, e_enc, W_pre_words, W_pre_scales, b_pre, out)
                 if q == 0 and turned_chunk is not None:
                     quantised = quantise_chunk(turned_chunk)
                     if copies is not None:
-                        apart = differences(copies, len(SHARED_TILES[h]) * TARGETS, behind_quantize=True)
+                        apart = differences(copies, len(tiles) * TARGETS, behind_quantize=True)
                 for older in (inserts or {}).get(q, []):
                     shared_extreme(*older)
             return quantised, apart
@@ -429,6 +431,7 @@ def tile_gnnlayer_pa_kernel(tc, x, e_enc, W_pre_words, W_pre_scales, b_pre, out)
         current = None
         graph_stats = {}
         in_flight = {}
+        tiles_of = {}
         for step in range(GROUPS):
             c, h = divmod(step, GROUPS_PER_CHUNK)
             b, part = divmod(c, CHUNKS_PER_GRAPH)
@@ -440,14 +443,17 @@ def tile_gnnlayer_pa_kernel(tc, x, e_enc, W_pre_words, W_pre_scales, b_pre, out)
                 graph_stats[b] = (s_moments, results)
             stats = graph_stats[b]
             shared = step < GROUPS - 1
-            rows = len(SHARED_TILES[h]) * TARGETS
-            other_rows = len(SHARED_TILES[1 - h]) * TARGETS
+            tiles_of[step] = ()
+            if shared:
+                tiles_of[step] = FEWER_SHARED_TILES if h == 0 and c % 2 == 1 else SHARED_TILES
+            tiles = tiles_of[step]
+            rows = len(tiles) * TARGETS
             if step - 1 in in_flight:
-                in_flight[step - 1].append(clip(in_flight[step - 1][1], other_rows))
-            banks, copies = messages(c, h, current[0], current[1], SHARED_TILES[h] if shared else ())
+                in_flight[step - 1].append(clip(in_flight[step - 1][1], len(tiles_of[step - 1]) * TARGETS))
+            banks, copies = messages(c, h, current[0], current[1], tiles)
             if step - SHARE_LAG in in_flight:
                 earlier = in_flight[step - SHARE_LAG]
-                earlier.append(larger_and_smaller(earlier[0], earlier[2], rows))
+                earlier.append(larger_and_smaller(earlier[0], earlier[2], len(tiles_of[step - SHARE_LAG]) * TARGETS))
             if shared and turned_chunk is None:
                 in_flight[step] = [copies, differences(copies, rows)]
             if step < GROUPS - 1:
@@ -455,11 +461,12 @@ def tile_gnnlayer_pa_kernel(tc, x, e_enc, W_pre_words, W_pre_scales, b_pre, out)
                 if step - SHARE_LAG in in_flight:
                     older_c, older_h = divmod(step - SHARE_LAG, GROUPS_PER_CHUNK)
                     older_b, older_part = divmod(older_c, CHUNKS_PER_GRAPH)
-                    older = (older_h, graph_stats[older_b], older_part * TARGETS)
+                    older = (older_h, graph_stats[older_b], older_part * TARGETS, tiles_of[step - SHARE_LAG])
                     inserts[2] = [(in_flight[step - SHARE_LAG][3], 0) + older]
                     inserts[3] = [(in_flight[step - SHARE_LAG][3], 1) + older]
                 quantised, apart = aggregate(
-                    banks, copies, h, stats, part * TARGETS, turned_chunk=turned_chunk, inserts=inserts, graph=b
+                    banks, copies, h, stats, part * TARGETS, turned_chunk=turned_chunk, inserts=inserts, graph=b,
+                    tiles=tiles,
                 )
                 if quantised is not None:
                     following = quantised
@@ -467,20 +474,20 @@ def tile_gnnlayer_pa_kernel(tc, x, e_enc, W_pre_words, W_pre_scales, b_pre, out)
                     in_flight[step] = [copies, apart]
             else:
                 last = in_flight[step - 1]
-                last.append(larger_and_smaller(last[0], last[2], other_rows))
+                last.append(larger_and_smaller(last[0], last[2], len(tiles_of[step - 1]) * TARGETS))
                 finish_moments(b, h - 1, stats)
                 aggregate(banks, copies, h, stats, part * TARGETS, extremes=False, graph=b)
                 finish_moments(b, h, stats)
                 summed_moments()
                 before_last = in_flight[step - SHARE_LAG][3]
                 inserts = {
-                    0: [(before_last, 0, h, stats, 0)],
-                    1: [(before_last, 1, h, stats, 0)],
-                    2: [(last[3], 0, h - 1, stats, part * TARGETS)],
+                    0: [(before_last, 0, h, stats, 0, tiles_of[step - SHARE_LAG])],
+                    1: [(before_last, 1, h, stats, 0, tiles_of[step - SHARE_LAG])],
+                    2: [(last[3], 0, h - 1, stats, part * TARGETS, tiles_of[step - 1])],
                 }
                 aggregate(banks, copies, h, stats, part * TARGETS, moments=False, inserts=inserts)
                 finish_store(b, h, stats)
-                shared_extreme(last[3], 1, h - 1, stats, part * TARGETS)
+                shared_extreme(last[3], 1, h - 1, stats, part * TARGETS, tiles_of[step - 1])
                 finish_store(b, h - 1, stats)
             if h == 0 and c + 1 < CHUNKS:
                 turned_chunk = turn_chunk(c + 1)
@@ -491,5 +498,8 @@ def tile_gnnlayer_pa_kernel(tc, x, e_enc, W_pre_words, W_pre_scales, b_pre, out)
                 b, part = divmod(c, CHUNKS_PER_GRAPH)
                 if part == CHUNKS_PER_GRAPH - 1 and done + FINISH_LAG == step:
                     finish_moments(b, h, graph_stats[b])
-                if part == CHUNKS_PER_GRAPH - 1 and done + FINISH_LAG + 1 == step:
+                store_step = done + FINISH_LAG + 1
+                if store_step % GROUPS_PER_CHUNK == 0 and store_step // GROUPS_PER_CHUNK + 1 < CHUNKS:
+                    store_step += 1
+                if part == CHUNKS_PER_GRAPH - 1 and store_step == step:
                     finish_store(b, h, graph_stats[b])

@@ -38,7 +38,7 @@ SHARED_TILES = (1, 2, 3)
 FEWER_SHARED_TILES = (2, 3)
 SHARE_LAG = 2
 HALF = N // 2
-TARGET_TERMS_STEP = 3
+TARGET_TERMS_STEPS = (3, 5)
 SUMMED_TILE = 0
 RAW_CHUNKS = 4
 
@@ -198,12 +198,13 @@ def tile_gnnlayer_pa_kernel(tc, x, e_enc, W_pre_words, W_pre_scales, b_pre, out)
             load_chunk(RAW_CHUNKS)
             return codes, scales
 
-        def target_terms():
-            nc.scalar.copy(out=bias_rows[:], in_=bias_rows_bf[:])
+        def turn_bias():
             bias_turned = psum_aux.tile([P, GROUP_TILES, P], F32, tag="bank")
             nc.tensor.transpose(bias_turned[:, 0, :], bias_rows[:], ident[:])
             nc.scalar.copy(out=bias_col[:], in_=bias_turned[:, 0, 0:F_TILES])
-            for h in range(GROUPS_PER_CHUNK):
+
+        def target_terms(h):
+            if True:
                 target_term = psum_aux.tile([P, GROUP_TILES, P], F32, tag="bank")
                 for q in range(GROUP_TILES):
                     for g in range(G):
@@ -352,11 +353,20 @@ def tile_gnnlayer_pa_kernel(tc, x, e_enc, W_pre_words, W_pre_scales, b_pre, out)
             nc.scalar.activation(out=results[:, tiles, 3, :], in_=variance[:, 0:count, :], func=ACT.Sqrt, bias=eps[:])
             nc.scalar.copy(out=results[:, tiles, 0, :], in_=moments[:, :, :, 1])
 
-        def finish_store(b, h, stats):
+        def add_base(b, h, stats):
+            tiles = slice(h * GROUP_TILES, (h + 1) * GROUP_TILES)
+            shifted = work.tile([P, GROUP_TILES, AGGREGATORS, N], F32)
+            nc.gpsimd.tensor_tensor(out=shifted[:], in0=stats[1][:, tiles, :, :], in1=base[:, tiles, b, :, :], op=ALU.add)
+            return shifted
+
+        def finish_store(b, h, stats, shifted=None):
             results = stats[1]
             turned = psum_aux.tile([P, GROUP_TILES, P], F32, tag="bank")
             for q in range(GROUP_TILES):
                 ft = h * GROUP_TILES + q
+                if shifted is not None:
+                    nc.tensor.transpose(turned[:, q, :], shifted[:, q, :, :].rearrange("p a i -> p (a i)"), ident[:])
+                    continue
                 nc.tensor.matmul(
                     turned[:, q, :],
                     lhsT=results[:, ft, :, :].rearrange("p a i -> p (a i)"),
@@ -431,6 +441,7 @@ def tile_gnnlayer_pa_kernel(tc, x, e_enc, W_pre_words, W_pre_scales, b_pre, out)
         current = None
         graph_stats = {}
         in_flight = {}
+        with_base = {}
         tiles_of = {}
         for step in range(GROUPS):
             c, h = divmod(step, GROUPS_PER_CHUNK)
@@ -445,15 +456,21 @@ def tile_gnnlayer_pa_kernel(tc, x, e_enc, W_pre_words, W_pre_scales, b_pre, out)
             shared = step < GROUPS - 1
             tiles_of[step] = ()
             if shared:
-                tiles_of[step] = FEWER_SHARED_TILES if h == 0 and c % 2 == 1 else SHARED_TILES
+                tiles_of[step] = FEWER_SHARED_TILES if h == 0 else SHARED_TILES
             tiles = tiles_of[step]
             rows = len(tiles) * TARGETS
             if step - 1 in in_flight:
                 in_flight[step - 1].append(clip(in_flight[step - 1][1], len(tiles_of[step - 1]) * TARGETS))
             banks, copies = messages(c, h, current[0], current[1], tiles)
+            if step == TARGET_TERMS_STEPS[0] - 1:
+                nc.scalar.copy(out=bias_rows[:], in_=bias_rows_bf[:])
             if step - SHARE_LAG in in_flight:
                 earlier = in_flight[step - SHARE_LAG]
                 earlier.append(larger_and_smaller(earlier[0], earlier[2], len(tiles_of[step - SHARE_LAG]) * TARGETS))
+            ready = step - FINISH_LAG - 1
+            ready_b = ready // (GROUPS_PER_CHUNK * CHUNKS_PER_GRAPH)
+            if 0 <= ready and ready_b < B - 2 and (ready // GROUPS_PER_CHUNK) % CHUNKS_PER_GRAPH == CHUNKS_PER_GRAPH - 1:
+                with_base[ready] = add_base(ready_b, ready % GROUPS_PER_CHUNK, graph_stats[ready_b])
             if shared and turned_chunk is None:
                 in_flight[step] = [copies, differences(copies, rows)]
             if step < GROUPS - 1:
@@ -491,8 +508,10 @@ def tile_gnnlayer_pa_kernel(tc, x, e_enc, W_pre_words, W_pre_scales, b_pre, out)
                 finish_store(b, h - 1, stats)
             if h == 0 and c + 1 < CHUNKS:
                 turned_chunk = turn_chunk(c + 1)
-            if step == TARGET_TERMS_STEP:
-                target_terms()
+            if step == TARGET_TERMS_STEPS[0] - 1:
+                turn_bias()
+            if step in TARGET_TERMS_STEPS:
+                target_terms(TARGET_TERMS_STEPS.index(step))
             for done in range(GROUPS - GROUPS_PER_CHUNK):
                 c, h = divmod(done, GROUPS_PER_CHUNK)
                 b, part = divmod(c, CHUNKS_PER_GRAPH)
@@ -501,5 +520,7 @@ def tile_gnnlayer_pa_kernel(tc, x, e_enc, W_pre_words, W_pre_scales, b_pre, out)
                 store_step = done + FINISH_LAG + 1
                 if store_step % GROUPS_PER_CHUNK == 0 and store_step // GROUPS_PER_CHUNK + 1 < CHUNKS:
                     store_step += 1
+                if b < B - 2:
+                    store_step = done - h + FINISH_LAG + 3
                 if part == CHUNKS_PER_GRAPH - 1 and store_step == step:
-                    finish_store(b, h, graph_stats[b])
+                    finish_store(b, h, graph_stats[b], with_base.get(done))

from contextlib import ExitStack

import concourse.mybir as mybir
from concourse.masks import make_identity

F32 = mybir.dt.float32
BF16 = mybir.dt.bfloat16
I32 = mybir.dt.int32
U32 = mybir.dt.uint32
U8 = mybir.dt.uint8
FP8X4 = mybir.dt.float8_e4m3fn_x4
FP4X4 = mybir.dt.float4_e2m1fn_x4
ALU = mybir.AluOpType
ACT = mybir.ActivationFunctionType
AXIS = mybir.AxisListType

B, N, C, F = 4, 32, 1024, 1024
EPS_STD = 1e-5
P = 128
PACK = 4
K_PASS = P * PACK
G = C // K_PASS
W_TARGET, W_SOURCE, W_EDGE = 0, G, 2 * G
F_TILES = F // P
CHUNK = 512
TARGETS = CHUNK // N
CHUNKS = B * N * N // CHUNK
CHUNKS_PER_GRAPH = CHUNKS // B
ROW_TILES = CHUNK // P
WORDS = K_PASS // 2
AGGREGATORS = 4
GROUP_TILES = CHUNK // P
GROUPS_PER_CHUNK = F_TILES // GROUP_TILES
GROUPS = CHUNKS * GROUPS_PER_CHUNK
MOMENTS = 3
FINISH_LAG = 2
SHARED_TILES = (1, 2, 3)
FEWER_SHARED_TILES = (2, 3)
SHARE_LAG = 2
HALF = N // 2
TARGET_TERMS_STEPS = (3, 5)
SUMMED_TILE = 0
RAW_CHUNKS = 4

FLOPS = 2 * (B * N * N + 2 * B * N) * C * F


def tile_gnnlayer_pa_kernel(tc, x, e_enc, W_pre_words, W_pre_scales, b_pre, out):
    nc = tc.nc
    with ExitStack() as ctx:
        ctx.enter_context(tc.manual_schedule())
        keep = ctx.enter_context(tc.tile_pool(name="keep", bufs=1))
        work = ctx.enter_context(tc.tile_pool(name="work", bufs=2))
        stream = ctx.enter_context(tc.tile_pool(name="stream", bufs=3))
        stage = ctx.enter_context(tc.tile_pool(name="stage", bufs=2))
        handover = ctx.enter_context(tc.tile_pool(name="handover", bufs=1))
        raw = ctx.enter_context(tc.tile_pool(name="raw", bufs=RAW_CHUNKS))
        psum_msg = ctx.enter_context(tc.psum_pool(name="psum_msg", bufs=4))
        psum_aux = ctx.enter_context(tc.psum_pool(name="psum_aux", bufs=4))

        x_raw = keep.tile([P, C], BF16)
        e_raw = {}
        by_source = keep.tile([P, 2, N, P], F32)
        plain_base = keep.tile([P, P], F32)
        zeros = keep.tile([P, 2, N], F32)
        w_words = [keep.tile([P, 3 * G, F], U8, align_bytes=64, name="w_words_%d" % h) for h in range(2)]
        w_scales = [keep.tile([P, 3 * G, F // 2], U8, align_bytes=64, name="w_scales_%d" % h) for h in range(2)]
        x_grouped = keep.tile([P, G, P, PACK], BF16, align_bytes=64)
        x_codes = keep.tile([P, G, P], U32, align_bytes=64)
        x_scales = keep.tile([P, G, P], U8, align_bytes=64)
        src_codes = keep.tile([P, B, G, CHUNK], U32, align_bytes=64)
        src_scales = keep.tile([P, B, G, CHUNK], U8, align_bytes=64)
        ident = keep.tile([P, P], F32)
        bias_rows_bf = keep.tile([P, P], BF16)
        bias_rows = keep.tile([P, P], F32)
        bias_col = keep.tile([P, F_TILES], F32)
        base = keep.tile([P, F_TILES, B, AGGREGATORS, N], F32)
        eps = keep.tile([P, 1], F32)
        idle_operand = keep.tile([P, CHUNK], BF16)
        warm = keep.tile([P, 1], F32)

        nc.gpsimd.memset(idle_operand[:], 0.0)
        for h in range(2):
            nc.vector.memset(w_scales[h][:].bitcast(I32), 0)
        nc.vector.memset(x_scales[:].bitcast(I32), 0)
        nc.vector.memset(bias_rows_bf[:], 0.0)
        nc.vector.memset(eps[:], EPS_STD)
        make_identity(nc, ident[:])
        nc.gpsimd.memset(base[:, :, :, 3, :], 0.0)
        nc.gpsimd.memset(zeros[:], 0.0)
        nc.scalar.activation(out=warm[:], in_=eps[:], func=ACT.Sqrt)

        nc.sync.dma_start(out=x_raw[:], in_=x.rearrange("b n c -> (b n) c"))
        edges = e_enc.rearrange("b i j c -> (b i j) c")

        def load_chunk(c):
            rows = raw.tile([P, ROW_TILES, C], BF16)
            for t in range(ROW_TILES):
                first_row = c * CHUNK + t * P
                nc.sync.dma_start(out=rows[:, t, :], in_=edges[first_row : first_row + P, :])
            e_raw[c] = rows

        def load_weights(first_group, groups, h):
            chosen = slice(first_group, first_group + groups)
            nc.sync.dma_start(
                out=w_words[h][:, chosen, :].bitcast(I32),
                in_=W_pre_words[chosen].rearrange("g p n -> p g n")[:, :, h * F : (h + 1) * F].bitcast(I32),
            )

        scale_rows = W_pre_scales.rearrange("g (m r) n -> r m g n", r=4)

        def load_scales(first_group, groups, h):
            chosen = slice(first_group, first_group + groups)
            for r in range(4):
                nc.sync.dma_start(
                    out=w_scales[h][r : P : 32, chosen, :].bitcast(I32),
                    in_=scale_rows[r][:, chosen, h * (F // 2) : (h + 1) * (F // 2)].bitcast(I32),
                )

        load_chunk(0)
        load_scales(W_SOURCE, 2 * G, 0)
        load_weights(W_SOURCE, 2 * G, 0)
        load_chunk(1)
        load_scales(W_SOURCE, 2 * G, 1)
        load_weights(W_SOURCE, 2 * G, 1)
        for h in range(2):
            load_scales(W_TARGET, G, h)
            load_weights(W_TARGET, G, h)
        nc.sync.dma_start(out=bias_rows_bf[0:F_TILES, :], in_=b_pre.rearrange("(t f) -> t f", f=P))
        for c in range(2, RAW_CHUNKS):
            load_chunk(c)

        def k_onto_partitions(rows_bf16, grouped):
            words = rows_bf16.bitcast(F32)
            turned = psum_aux.tile([P, G, 2, P], F32, tag="bank")
            for g in range(G):
                for u in range(2):
                    nc.tensor.transpose(
                        turned[:, g, u, :], words[:, g * WORDS + u : (g + 1) * WORDS : 2], ident[:]
                    )
            nc.scalar.copy(out=grouped.bitcast(F32), in_=turned[:].rearrange("p g u r -> p g r u"))

        def keep_clock_up(matmuls):
            bank = psum_msg.tile([P, CHUNK], F32)
            for n in range(matmuls):
                nc.tensor.matmul(bank[:], lhsT=idle_operand[:, 0:P], rhs=idle_operand[:], start=True, stop=True)

        def weight(group, ft):
            h, q = divmod(ft, GROUP_TILES)
            return dict(
                lhsT=w_words[h][:, group, 2 * P * q : 2 * P * (q + 1)].bitcast(FP4X4),
                lhsT_scale=w_scales[h][:, group, P * q : P * (q + 1)],
            )

        def repeat_sources(b):
            nodes = slice(b * N, (b + 1) * N)
            nc.vector.tensor_copy(
                out=src_codes[:, b, :, :].bitcast(I32).rearrange("p g (i j) -> p g i j", j=N),
                in_=x_codes[:, :, nodes].bitcast(I32).unsqueeze(2).to_broadcast([P, G, TARGETS, N]),
            )
            nc.vector.tensor_copy(
                out=src_scales[:, b, :, :].bitcast(I32).rearrange("p g (i w) -> p g i w", w=N // 4),
                in_=x_scales[:, :, nodes].bitcast(I32).unsqueeze(2).to_broadcast([P, G, TARGETS, N // 4]),
            )

        def turn_chunk(c):
            grouped = handover.tile([P, G, CHUNK, PACK], BF16, align_bytes=64, tag="turn")
            for t in range(ROW_TILES):
                k_onto_partitions(e_raw[c][:, t, :], grouped[:, :, t * P : (t + 1) * P, :])
            if c + RAW_CHUNKS < CHUNKS:
                load_chunk(c + RAW_CHUNKS)
            return grouped

        def quantise_chunk(grouped):
            codes = work.tile([P, G, CHUNK], U32, align_bytes=64)
            scales = work.tile([P, G, CHUNK], U8, align_bytes=64)
            nc.vector.quantize_mx(
                out=codes[:].rearrange("p g e -> p (g e)").bitcast(FP8X4),
                scales=scales[:].rearrange("p g e -> p (g e)"),
                in_=grouped[:].rearrange("p g e t -> p (g e t)"),
            )
            return codes, scales

        def first_chunk():
            codes = work.tile([P, G, CHUNK], U32, align_bytes=64)
            scales = work.tile([P, G, CHUNK], U8, align_bytes=64)
            for t in range(ROW_TILES):
                part = keep.tile([P, G, P, PACK], BF16, align_bytes=64, name="first_rows_%d" % t)
                k_onto_partitions(e_raw[0][:, t, :], part[:])
                keep_clock_up(1 if t < ROW_TILES - 1 else 2)
                rows = slice(t * P, (t + 1) * P)
                for g in range(G):
                    nc.vector.quantize_mx(
                        out=codes[:, g, rows].bitcast(FP8X4),
                        scales=scales[:, g, rows],
                        in_=part[:, g, :, :].rearrange("p e t -> p (e t)"),
                    )
            load_chunk(RAW_CHUNKS)
            return codes, scales

        def turn_bias():
            bias_turned = psum_aux.tile([P, GROUP_TILES, P], F32, tag="bank")
            nc.tensor.transpose(bias_turned[:, 0, :], bias_rows[:], ident[:])
            nc.scalar.copy(out=bias_col[:], in_=bias_turned[:, 0, 0:F_TILES])

        def target_terms(h):
            if True:
                target_term = psum_aux.tile([P, GROUP_TILES, P], F32, tag="bank")
                for q in range(GROUP_TILES):
                    for g in range(G):
                        nc.tensor.matmul_mx(
                            out=target_term[:, q, :],
                            rhs=x_codes[:, g, :].bitcast(FP8X4),
                            rhs_scale=x_scales[:, g, :],
                            start=(g == 0),
                            stop=(g == G - 1),
                            **weight(W_TARGET + g, h * GROUP_TILES + q),
                        )
                for q in range(GROUP_TILES):
                    ft = h * GROUP_TILES + q
                    nc.scalar.activation(
                        out=base[:, ft, :, 0:3, :],
                        in_=target_term[:, q, :]
                        .rearrange("p (b i) -> p b i", i=N)
                        .unsqueeze(2)
                        .to_broadcast([P, B, 3, N]),
                        func=ACT.Identity,
                        bias=bias_col[:, ft : ft + 1],
                        scale=1.0,
                    )
                    if ft == SUMMED_TILE:
                        nc.scalar.activation(
                            out=plain_base[:],
                            in_=target_term[:, q, :],
                            func=ACT.Identity,
                            bias=bias_col[:, ft : ft + 1],
                            scale=1.0,
                        )

        def messages(c, h, codes, scales, tiles):
            b = c // CHUNKS_PER_GRAPH
            moving = [(W_SOURCE + g, src_codes[:, b, g, :], src_scales[:, b, g, :]) for g in range(G)]
            moving += [(W_EDGE + g, codes[:, g, :], scales[:, g, :]) for g in range(G)]
            banks = []
            copies = None
            if tiles:
                copies = stream.tile([P, len(tiles) * TARGETS, N], F32)
            for q in range(GROUP_TILES):
                bank = psum_msg.tile([P, CHUNK], F32)
                for n, (group, rhs, rhs_scale) in enumerate(moving):
                    nc.tensor.matmul_mx(
                        out=bank[:],
                        rhs=rhs.bitcast(FP8X4),
                        rhs_scale=rhs_scale,
                        start=(n == 0),
                        stop=(n == len(moving) - 1),
                        **weight(group, h * GROUP_TILES + q),
                    )
                if q in tiles:
                    slot = tiles.index(q)
                    nc.scalar.copy(
                        out=copies[:, slot * TARGETS : (slot + 1) * TARGETS, :].rearrange("p i j -> p (i j)"),
                        in_=bank[:],
                    )
                banks.append(bank)
            return banks, copies

        def differences(copies, rows, behind_quantize=False):
            if behind_quantize:
                apart = handover.tile([P, rows, HALF], F32, align_bytes=64, tag="turn")
            else:
                apart = stage.tile([P, rows, HALF], F32)
            nc.gpsimd.tensor_tensor(
                out=apart[:], in0=copies[:, :, HALF:N], in1=copies[:, :, 0:HALF], op=ALU.subtract
            )
            return apart

        def clip(apart, rows):
            clipped = stage.tile([P, rows, HALF], F32)
            nc.scalar.activation(out=clipped[:], in_=apart[:], func=ACT.Relu)
            return clipped

        def larger_and_smaller(copies, clipped, rows):
            sorted_pairs = stage.tile([P, 2, rows, HALF], F32)
            nc.gpsimd.tensor_tensor(
                out=sorted_pairs[:, 0, :, :], in0=copies[:, :, 0:HALF], in1=clipped[:], op=ALU.add
            )
            nc.gpsimd.tensor_tensor(
                out=sorted_pairs[:, 1, :, :], in0=copies[:, :, HALF:N], in1=clipped[:], op=ALU.subtract
            )
            return sorted_pairs

        def shared_extreme(sorted_pairs, smaller, h, stats, first_target, shared_tiles):
            results = stats[1]
            tiles = slice(h * GROUP_TILES + shared_tiles[0], h * GROUP_TILES + shared_tiles[-1] + 1)
            targets = slice(first_target, first_target + TARGETS)
            nc.vector.tensor_reduce(
                out=results[:, tiles, 2 - smaller, targets],
                in_=sorted_pairs[:, smaller, :, :].rearrange("p (n i) k -> p n i k", i=TARGETS),
                axis=AXIS.X,
                op=(ALU.max, ALU.min)[smaller],
            )

        def aggregate(
            banks, copies, h, stats, first_target, moments=True, extremes=True, turned_chunk=None, inserts=None, graph=0,
            tiles=(),
        ):
            s_moments, results = stats
            targets = slice(first_target, first_target + TARGETS)
            quantised = None
            apart = None
            for q in range(GROUP_TILES):
                ft = h * GROUP_TILES + q
                s = banks[q][:].rearrange("p (i j) -> p i j", j=N)
                shared = q in tiles
                if shared:
                    slot = tiles.index(q)
                    s = copies[:, slot * TARGETS : (slot + 1) * TARGETS, :]
                summed = ft == SUMMED_TILE
                for pair in range(TARGETS // 2 if moments and not summed else 0):
                    first = MOMENTS * (first_target + 2 * pair)
                    nc.vector.bn_stats(
                        out=s_moments[:, ft, first : first + 2 * MOMENTS],
                        in_=s[:, 2 * pair : 2 * pair + 2, :].rearrange("p i j -> p j i"),
                    )
                if (moments if summed else extremes) and not shared:
                    nc.vector.tensor_reduce(out=results[:, ft, 2, targets], in_=s, axis=AXIS.X, op=ALU.max)
                    nc.vector.tensor_reduce(out=results[:, ft, 1, targets], in_=s, axis=AXIS.X, op=ALU.min)
                if summed and moments:
                    columns = slice(graph * N + first_target, graph * N + first_target + TARGETS)
                    source_first = banks[q][:].rearrange("p (i j) -> p j i", j=N)
                    nc.scalar.copy(out=by_source[:, 0, :, columns], in_=source_first)
                    nc.scalar.activation(out=by_source[:, 1, :, columns], in_=source_first, func=ACT.Square)
                if q == 0 and turned_chunk is not None:
                    quantised = quantise_chunk(turned_chunk)
                    if copies is not None:
                        apart = differences(copies, len(tiles) * TARGETS, behind_quantize=True)
                for older in (inserts or {}).get(q, []):
                    shared_extreme(*older)
            return quantised, apart

        def finish_moments(b, h, stats):
            s_moments, results = stats
            first = h * GROUP_TILES
            if first == SUMMED_TILE:
                nc.scalar.copy(out=results[:, first, 0:AGGREGATORS:3, :], in_=zeros[:])
                first += 1
            tiles = slice(first, (h + 1) * GROUP_TILES)
            moments = s_moments[:, tiles, :].rearrange("p q (i m) -> p q i m", m=MOMENTS)
            variance = work.tile([P, GROUP_TILES, N], F32)
            count = (h + 1) * GROUP_TILES - first
            nc.scalar.activation(out=variance[:, 0:count, :], in_=moments[:, :, :, 2], func=ACT.Relu, scale=1.0 / N)
            nc.scalar.activation(out=results[:, tiles, 3, :], in_=variance[:, 0:count, :], func=ACT.Sqrt, bias=eps[:])
            nc.scalar.copy(out=results[:, tiles, 0, :], in_=moments[:, :, :, 1])

        def add_base(b, h, stats):
            tiles = slice(h * GROUP_TILES, (h + 1) * GROUP_TILES)
            shifted = work.tile([P, GROUP_TILES, AGGREGATORS, N], F32)
            nc.gpsimd.tensor_tensor(out=shifted[:], in0=stats[1][:, tiles, :, :], in1=base[:, tiles, b, :, :], op=ALU.add)
            return shifted

        def finish_store(b, h, stats, shifted=None):
            results = stats[1]
            turned = psum_aux.tile([P, GROUP_TILES, P], F32, tag="bank")
            for q in range(GROUP_TILES):
                ft = h * GROUP_TILES + q
                if shifted is not None:
                    nc.tensor.transpose(turned[:, q, :], shifted[:, q, :, :].rearrange("p a i -> p (a i)"), ident[:])
                    continue
                nc.tensor.matmul(
                    turned[:, q, :],
                    lhsT=results[:, ft, :, :].rearrange("p a i -> p (a i)"),
                    rhs=ident[:],
                    is_transpose=True,
                    start=True,
                    stop=False,
                )
                nc.tensor.matmul(
                    turned[:, q, :],
                    lhsT=base[:, ft, b, :, :].rearrange("p a i -> p (a i)"),
                    rhs=ident[:],
                    is_transpose=True,
                    start=False,
                    stop=True,
                )
            rows = work.tile([P, CHUNK], F32)
            nc.scalar.copy(out=rows[:], in_=turned[:].rearrange("p q f -> p (q f)"))
            for a in range(AGGREGATORS):
                first = a * F + h * CHUNK
                skip = P if h * GROUP_TILES == SUMMED_TILE and a in (0, 3) else 0
                nc.sync.dma_start(
                    out=out[b, :, first + skip : first + CHUNK], in_=rows[a * N : (a + 1) * N, skip:CHUNK]
                )

        def summed_moments():
            sums = psum_aux.tile([P, GROUP_TILES, P], F32, tag="bank")
            for k in range(2):
                for j in range(N):
                    nc.tensor.matmul(
                        sums[:, k, :],
                        lhsT=by_source[:, k, j, :],
                        rhs=ident[:],
                        is_transpose=True,
                        start=(j == 0),
                        stop=(j == N - 1),
                    )
            nc.tensor.transpose(sums[:, 2, :], plain_base[:], ident[:])
            pieces = keep.tile([P, 8, P], F32)
            mean_s, mean_squared, second, base_turned, variance, mean, clipped, deviation = [
                pieces[:, n, :] for n in range(8)
            ]
            nc.scalar.activation(out=mean_s, in_=sums[:, 0, :], func=ACT.Copy, scale=1.0 / N)
            nc.scalar.activation(out=mean_squared, in_=sums[:, 0, :], func=ACT.Square, scale=1.0 / N)
            nc.scalar.activation(out=second, in_=sums[:, 1, :], func=ACT.Copy, scale=1.0 / N)
            nc.scalar.copy(out=base_turned, in_=sums[:, 2, :])
            nc.gpsimd.tensor_tensor(out=variance, in0=second, in1=mean_squared, op=ALU.subtract)
            nc.gpsimd.tensor_tensor(out=mean, in0=mean_s, in1=base_turned, op=ALU.add)
            nc.scalar.activation(out=clipped, in_=variance, func=ACT.Relu)
            nc.scalar.activation(out=deviation, in_=clipped, func=ACT.Sqrt, bias=eps[:])
            all_targets = out.rearrange("b i f -> (b i) f")
            nc.sync.dma_start(out=all_targets[:, SUMMED_TILE * P : (SUMMED_TILE + 1) * P], in_=mean)
            first = 3 * F + SUMMED_TILE * P
            nc.sync.dma_start(out=all_targets[:, first : first + P], in_=deviation)

        keep_clock_up(3)
        k_onto_partitions(x_raw[:], x_grouped[:])
        keep_clock_up(1)
        nc.vector.quantize_mx(
            out=x_codes[:].rearrange("p g r -> p (g r)").bitcast(FP8X4),
            scales=x_scales[:].rearrange("p g r -> p (g r)"),
            in_=x_grouped[:].rearrange("p g r t -> p (g r t)"),
        )

        for b in range(B // 2):
            repeat_sources(b)

        following = first_chunk()
        for b in range(B // 2, B):
            repeat_sources(b)
        turned_chunk = None
        current = None
        graph_stats = {}
        in_flight = {}
        with_base = {}
        tiles_of = {}
        for step in range(GROUPS):
            c, h = divmod(step, GROUPS_PER_CHUNK)
            b, part = divmod(c, CHUNKS_PER_GRAPH)
            if h == 0:
                current = following
            if h == 0 and part == 0:
                s_moments = work.tile([P, F_TILES, MOMENTS * N], F32)
                results = work.tile([P, F_TILES, AGGREGATORS, N], F32)
                graph_stats[b] = (s_moments, results)
            stats = graph_stats[b]
            shared = step < GROUPS - 1
            tiles_of[step] = ()
            if shared:
                tiles_of[step] = FEWER_SHARED_TILES if h == 0 else SHARED_TILES
            tiles = tiles_of[step]
            rows = len(tiles) * TARGETS
            if step - 1 in in_flight:
                in_flight[step - 1].append(clip(in_flight[step - 1][1], len(tiles_of[step - 1]) * TARGETS))
            banks, copies = messages(c, h, current[0], current[1], tiles)
            if step == TARGET_TERMS_STEPS[0] - 1:
                nc.scalar.copy(out=bias_rows[:], in_=bias_rows_bf[:])
            if step - SHARE_LAG in in_flight:
                earlier = in_flight[step - SHARE_LAG]
                earlier.append(larger_and_smaller(earlier[0], earlier[2], len(tiles_of[step - SHARE_LAG]) * TARGETS))
            ready = step - FINISH_LAG - 1
            ready_b = ready // (GROUPS_PER_CHUNK * CHUNKS_PER_GRAPH)
            if 0 <= ready and ready_b < B - 2 and (ready // GROUPS_PER_CHUNK) % CHUNKS_PER_GRAPH == CHUNKS_PER_GRAPH - 1:
                with_base[ready] = add_base(ready_b, ready % GROUPS_PER_CHUNK, graph_stats[ready_b])
            if shared and turned_chunk is None:
                in_flight[step] = [copies, differences(copies, rows)]
            if step < GROUPS - 1:
                inserts = {}
                if step - SHARE_LAG in in_flight:
                    older_c, older_h = divmod(step - SHARE_LAG, GROUPS_PER_CHUNK)
                    older_b, older_part = divmod(older_c, CHUNKS_PER_GRAPH)
                    older = (older_h, graph_stats[older_b], older_part * TARGETS, tiles_of[step - SHARE_LAG])
                    inserts[2] = [(in_flight[step - SHARE_LAG][3], 0) + older]
                    inserts[3] = [(in_flight[step - SHARE_LAG][3], 1) + older]
                quantised, apart = aggregate(
                    banks, copies, h, stats, part * TARGETS, turned_chunk=turned_chunk, inserts=inserts, graph=b,
                    tiles=tiles,
                )
                if quantised is not None:
                    following = quantised
                    turned_chunk = None
                    in_flight[step] = [copies, apart]
            else:
                last = in_flight[step - 1]
                last.append(larger_and_smaller(last[0], last[2], len(tiles_of[step - 1]) * TARGETS))
                finish_moments(b, h - 1, stats)
                aggregate(banks, copies, h, stats, part * TARGETS, extremes=False, graph=b)
                finish_moments(b, h, stats)
                summed_moments()
                before_last = in_flight[step - SHARE_LAG][3]
                inserts = {
                    0: [(before_last, 0, h, stats, 0, tiles_of[step - SHARE_LAG])],
                    1: [(before_last, 1, h, stats, 0, tiles_of[step - SHARE_LAG])],
                    2: [(last[3], 0, h - 1, stats, part * TARGETS, tiles_of[step - 1])],
                }
                aggregate(banks, copies, h, stats, part * TARGETS, moments=False, inserts=inserts)
                finish_store(b, h, stats)
                shared_extreme(last[3], 1, h - 1, stats, part * TARGETS, tiles_of[step - 1])
                finish_store(b, h - 1, stats)
            if h == 0 and c + 1 < CHUNKS:
                turned_chunk = turn_chunk(c + 1)
            if step == TARGET_TERMS_STEPS[0] - 1:
                turn_bias()
            if step in TARGET_TERMS_STEPS:
                target_terms(TARGET_TERMS_STEPS.index(step))
            for done in range(GROUPS - GROUPS_PER_CHUNK):
                c, h = divmod(done, GROUPS_PER_CHUNK)
                b, part = divmod(c, CHUNKS_PER_GRAPH)
                if part == CHUNKS_PER_GRAPH - 1 and done + FINISH_LAG == step:
                    finish_moments(b, h, graph_stats[b])
                store_step = done + FINISH_LAG + 1
                if store_step % GROUPS_PER_CHUNK == 0 and store_step // GROUPS_PER_CHUNK + 1 < CHUNKS:
                    store_step += 1
                if b < B - 2:
                    store_step = done - h + FINISH_LAG + 3
                if part == CHUNKS_PER_GRAPH - 1 and store_step == step:
                    finish_store(b, h, graph_stats[b], with_base.get(done))
